import numpy as np
import ml_dtypes


def mxq(x, axis, fmt="e4m3"):
    dtype, down = {"e4m3": (ml_dtypes.float8_e4m3fn, 7), "e5m2": (ml_dtypes.float8_e5m2, 14)}[fmt]
    v = np.moveaxis(np.asarray(x, np.float32).astype(ml_dtypes.bfloat16).astype(np.float64), axis, -1)
    blocks = v.reshape(v.shape[:-1] + (-1, 32))
    amax = np.abs(blocks).max(-1, keepdims=True)
    byte = np.maximum(np.where(amax > 0, np.frexp(amax)[1] - 1 + 127, 0) - down, 1)
    scale = np.exp2(byte - 127.0)
    codes = (blocks / scale).astype(np.float32).astype(dtype).astype(np.float64)
    return np.moveaxis((codes * scale).reshape(v.shape), -1, axis)


WIDE = False


def mx_kscale(k):
    if not WIDE:
        return np.ones(k)
    levels = np.array([10, -10, 5, -5, 0])
    a = np.random.permutation(np.resize(levels, k // 512 * 4)).reshape(k // 512, 4)
    idx = np.arange(k)
    return np.exp2(a[idx // 512, idx % 128 // 32])


BF16 = ml_dtypes.bfloat16


def bf(x):
    return np.asarray(x, np.float32).astype(BF16)


def f64(x):
    return np.asarray(x).astype(np.float64)


B, CIN, COUT, H, W, KERNEL, PAD, GRID_SIZE, SPLINE_ORDER = 2, 64, 256, 30, 30, 1, 1, 5, 3
GRID_RANGE = (-1.0, 1.0)
GS = GRID_SIZE + SPLINE_ORDER
HP, WP = H + 2 * PAD, W + 2 * PAD
HO, WO = HP - KERNEL + 1, WP - KERNEL + 1
KK = KERNEL * KERNEL
CG = CIN * GS
CB = 32 // GS
HK = (GRID_RANGE[1] - GRID_RANGE[0]) / GRID_SIZE


def b_spline_basis(x, grid, order):
    x = x[..., None]
    bases = ((x >= grid[:-1]) & (x < grid[1:])).astype(np.float64)
    for k in range(1, order + 1):
        left = (x - grid[: -(k + 1)]) / (grid[k:-1] - grid[: -(k + 1)]) * bases[..., :-1]
        right = (grid[k + 1:] - x) / (grid[k + 1:] - grid[1:-k]) * bases[..., 1:]
        bases = left + right
    return bases


def setup_inputs():
    s = np.asarray(mx_kscale(CG)).reshape(CIN // CB, CB * GS).min(axis=1)
    x = np.random.standard_normal((B, CIN, H, W))
    sw = np.random.standard_normal((COUT, CIN, GS, KERNEL, KERNEL)) * 2.4 / np.sqrt(CIN * KK)
    sc = np.random.random_sample((COUT, CIN))
    if s.min() < 1:
        c = int(np.argmin(s))
        ch = slice(CB * c, CB * c + CB)
        lo = GRID_RANGE[0] - SPLINE_ORDER * HK + HK / 32
        hi = GRID_RANGE[1] + SPLINE_ORDER * HK - HK / 32
        x[:, ch] = np.where(x[:, ch] < 0, lo, hi)
        sw[:, ch, 0] *= 2.0 ** (5 * SPLINE_ORDER + 4)
        sw[:, ch, GS - 1] *= 2.0 ** (5 * SPLINE_ORDER + 4)
    return {"x": bf(x), "spline_weight": bf(sw), "spline_scaler": bf(sc)}


def reference(x, spline_weight, spline_scaler):
    h = (GRID_RANGE[1] - GRID_RANGE[0]) / GRID_SIZE
    grid = np.arange(-SPLINE_ORDER, GRID_SIZE + SPLINE_ORDER + 1).astype(np.float64) * h + GRID_RANGE[0]
    xp = np.pad(f64(x), ((0, 0), (0, 0), (PAD, PAD), (PAD, PAD)))
    bases = b_spline_basis(xp, grid, SPLINE_ORDER)
    bq = mxq(bases.transpose(0, 2, 3, 1, 4).reshape(B, HP, WP, CG), 3, "e4m3")
    patches = np.stack([bq[:, i:i + HO, j:j + WO, :] for i in range(KERNEL) for j in range(KERNEL)], axis=3)
    w = f64(spline_weight) * f64(spline_scaler)[:, :, None, None, None]
    wq = mxq(w.transpose(3, 4, 1, 2, 0).reshape(KK * CG, COUT), 0, "e4m3")
    out = patches.reshape(B * HO * WO, KK * CG) @ wq
    return out.reshape(B, HO, WO, COUT).transpose(0, 3, 1, 2)

@@ -1,0 +1,169 @@
+import math
+
+import concourse.mybir as mybir
+from concourse.masks import make_identity
+
+F32 = mybir.dt.float32
+BF16 = mybir.dt.bfloat16
+I32 = mybir.dt.int32
+U32 = mybir.dt.uint32
+U8 = mybir.dt.uint8
+FP8X4 = mybir.dt.float8_e4m3fn_x4
+ALU = mybir.AluOpType
+ACT = mybir.ActivationFunctionType
+
+P = 128
+PACK = 4
+BATCH, CIN, COUT, SIDE = 2, 64, 256, 30
+BASES = 8
+GROUPS = CIN // PACK
+PADDED = SIDE + 2
+HALVES = 2
+HALF_ROWS = SIDE // HALVES
+HALF_PADDED_ROWS = PADDED // HALVES
+N_TILE = HALF_PADDED_ROWS * PADDED
+O_TILES = COUT // P
+INV_SPACING = 2.5
+OUTER_ROOT = math.sqrt(1.0 / 6.0)
+INNER_ROOT = math.sqrt(2.0 / 3.0)
+
+FLOPS = 2 * BATCH * PADDED * PADDED * CIN * BASES * COUT
+
+
+def spline_basis(nc, work, x_view, shift, out_view, rows):
+    width = x_view.shape[1] * x_view.shape[2]
+    dist = work.tile([P, width], F32)
+    nc.scalar.activation(
+        out=dist[:].rearrange("p (w j) -> p w j", j=PACK), in_=x_view, func=ACT.Abs, bias=shift, scale=INV_SPACING
+    )
+    outer = work.tile([P, width], F32)
+    nc.vector.tensor_scalar(out=outer[:], in0=dist[:], scalar1=2.0, scalar2=-2.0, op0=ALU.min, op1=ALU.add)
+    inner = work.tile([P, width], F32)
+    nc.vector.tensor_scalar(out=inner[:], in0=dist[:], scalar1=1.0, scalar2=-1.0, op0=ALU.min, op1=ALU.add)
+    outer_sq = work.tile([P, width], F32)
+    nc.scalar.activation(out=outer_sq[:], in_=outer[:], func=ACT.Square, scale=OUTER_ROOT)
+    inner_sq = work.tile([P, width], F32)
+    nc.scalar.activation(out=inner_sq[:], in_=inner[:], func=ACT.Square, scale=INNER_ROOT)
+    outer_cube = work.tile([P, width], F32)
+    nc.vector.tensor_tensor(out=outer_cube[:], in0=outer[:], in1=outer_sq[:], op=ALU.mult)
+    inner_cube = work.tile([P, width], F32)
+    nc.vector.tensor_tensor(out=inner_cube[:], in0=inner[:], in1=inner_sq[:], op=ALU.mult)
+    nc.vector.tensor_tensor(
+        out=out_view,
+        in0=inner_cube[:].rearrange("p (r c) -> p r c", r=rows),
+        in1=outer_cube[:].rearrange("p (r c) -> p r c", r=rows),
+        op=ALU.subtract,
+    )
+
+
+def tile_kanv2d_s_kernel(tc, x, spline_weight, spline_scaler, out):
+    nc = tc.nc
+    with (
+        tc.tile_pool(name="keep", bufs=1) as keep,
+        tc.tile_pool(name="work", bufs=3) as work,
+        tc.tile_pool(name="results", bufs=4) as results,
+        tc.psum_pool(name="flip", bufs=1) as flip,
+        tc.psum_pool(name="sums", bufs=6) as sums,
+    ):
+        x_sb = keep.tile([P, BATCH, PACK, SIDE * SIDE], BF16)
+
+        def load_image(n):
+            for g in range(BASES):
+                nc.sync.dma_start(
+                    out=x_sb[g:P:BASES, n, :, :], in_=x[n].rearrange("(q j) h w -> q j (h w)", j=PACK)
+                )
+
+        load_image(0)
+        weight_sb = keep.tile([P, O_TILES, CIN * BASES], BF16)
+        nc.scalar.dma_start(out=weight_sb[:], in_=spline_weight.rearrange("(t p) i g k l -> p t (i g k l)", p=P))
+        scaler_sb = keep.tile([P, O_TILES, CIN], BF16)
+        nc.scalar.dma_start(out=scaler_sb[:], in_=spline_scaler.rearrange("(t p) i -> p t i", p=P))
+        load_image(1)
+
+        partition_index = keep.tile([P, 1], I32)
+        nc.gpsimd.iota(partition_index[:], pattern=[[0, 1]], base=0, channel_multiplier=1)
+        basis_index = keep.tile([P, 1], I32)
+        nc.vector.tensor_single_scalar(out=basis_index[:], in_=partition_index[:], scalar=BASES - 1, op=ALU.bitwise_and)
+        shift = keep.tile([P, 1], F32)
+        nc.vector.tensor_scalar(
+            out=shift[:], in0=basis_index[:], scalar1=-1.0, scalar2=(BASES - 1) / 2.0, op0=ALU.mult, op1=ALU.add
+        )
+
+        basis = keep.tile([P, BATCH, PADDED, PADDED, PACK], BF16, align_bytes=64)
+        zero_x = keep.tile([P, 1, PACK], BF16)
+        nc.vector.memset(zero_x[:], 0.0)
+        pad_basis = keep.tile([P, 1, PACK], BF16)
+        spline_basis(nc, work, zero_x[:], shift[:], pad_basis[:], 1)
+        pad_value = pad_basis[:, :, 0:1]
+        for row in (0, PADDED - 1):
+            nc.vector.tensor_copy(
+                out=basis[:, :, row, :, :].rearrange("p n c j -> p n (c j)"),
+                in_=pad_value.to_broadcast([P, BATCH, PADDED * PACK]),
+            )
+        for col in (0, PADDED - 1):
+            nc.vector.tensor_copy(
+                out=basis[:, :, :, col, :], in_=pad_value.unsqueeze(3).to_broadcast([P, BATCH, PADDED, PACK])
+            )
+
+        scaled = keep.tile([P, O_TILES, PACK, P], BF16)
+        for t in range(O_TILES):
+            nc.vector.tensor_tensor(
+                out=scaled[:, t, :, :].rearrange("p j (q g) -> p j q g", g=BASES),
+                in0=weight_sb[:, t, :].rearrange("p (q j g) -> p j q g", j=PACK, g=BASES),
+                in1=scaler_sb[:, t, :]
+                .rearrange("p (q j) -> p j q", j=PACK)
+                .unsqueeze(3)
+                .to_broadcast([P, PACK, GROUPS, BASES]),
+                op=ALU.mult,
+            )
+        identity = keep.tile([P, P], BF16)
+        make_identity(nc, identity[:])
+        flipped = flip.tile([P, O_TILES, PACK, P], BF16)
+        for t in range(O_TILES):
+            for j in range(PACK):
+                nc.tensor.transpose(flipped[:, t, j, :], scaled[:, t, j, :], identity[:])
+        w_grouped = keep.tile([P, O_TILES, P, PACK], BF16, align_bytes=64)
+        nc.vector.tensor_copy(out=w_grouped[:], in_=flipped[:].rearrange("p t j o -> p t o j"))
+        w_codes = keep.tile([P, COUT], U32, align_bytes=64)
+        w_scales = keep.tile([P, COUT], U8, align_bytes=64)
+        nc.vector.quantize_mx(
+            out=w_codes[:].bitcast(FP8X4), scales=w_scales[:], in_=w_grouped[:].rearrange("p t o j -> p (t o j)")
+        )
+
+        b_codes = keep.tile([P, BATCH, HALVES, N_TILE], U32, align_bytes=64)
+        b_scales = keep.tile([P, BATCH, HALVES, N_TILE], U8, align_bytes=64)
+        for n in range(BATCH):
+            for h in range(HALVES):
+                pixels = slice(h * HALF_ROWS * SIDE, (h + 1) * HALF_ROWS * SIDE)
+                first_row = 1 + h * HALF_ROWS
+                spline_basis(
+                    nc,
+                    work,
+                    x_sb[:, n, :, pixels].rearrange("p j w -> p w j"),
+                    shift[:],
+                    basis[:, n, first_row : first_row + HALF_ROWS, 1 : 1 + SIDE, :].rearrange("p r c j -> p r (c j)"),
+                    HALF_ROWS,
+                )
+                padded_rows = slice(h * HALF_PADDED_ROWS, (h + 1) * HALF_PADDED_ROWS)
+                nc.vector.quantize_mx(
+                    out=b_codes[:, n, h, :].bitcast(FP8X4),
+                    scales=b_scales[:, n, h, :],
+                    in_=basis[:, n, padded_rows, :, :].rearrange("p r c j -> p (r c j)"),
+                )
+                for t in range(O_TILES):
+                    o_cols = slice(t * P, (t + 1) * P)
+                    acc = sums.tile([P, N_TILE], F32)
+                    nc.tensor.matmul_mx(
+                        out=acc[:],
+                        lhsT=w_codes[:, o_cols].bitcast(FP8X4),
+                        lhsT_scale=w_scales[:, o_cols],
+                        rhs=b_codes[:, n, h, :].bitcast(FP8X4),
+                        rhs_scale=b_scales[:, n, h, :],
+                        start=True,
+                        stop=True,
+                    )
+                    result = results.tile([P, N_TILE], F32)
+                    nc.scalar.copy(out=result[:], in_=acc[:])
+                    nc.sync.dma_start(
+                        out=out[n, o_cols, padded_rows, :].rearrange("o y z -> o (y z)"), in_=result[:]
+                    )

@@ -18,11 +18,13 @@ BATCH, CIN, COUT, SIDE = 2, 64, 256, 30
 BASES = 8
 GROUPS = CIN // PACK
 PADDED = SIDE + 2
-HALVES = 2
-HALF_ROWS = SIDE // HALVES
-HALF_PADDED_ROWS = PADDED // HALVES
-N_TILE = HALF_PADDED_ROWS * PADDED
+CHUNK_ROWS = 8
+CHUNKS_PER_IMAGE = PADDED // CHUNK_ROWS
+CHUNKS = BATCH * CHUNKS_PER_IMAGE
+N_TILE = CHUNK_ROWS * PADDED
+WIDTH = CHUNK_ROWS * SIDE * PACK
 O_TILES = COUT // P
+WEIGHTS_STEP = 1
 INV_SPACING = 2.5
 OUTER_ROOT = math.sqrt(1.0 / 6.0)
 INNER_ROOT = math.sqrt(2.0 / 3.0)
@@ -30,29 +32,54 @@ INNER_ROOT = math.sqrt(2.0 / 3.0)
 FLOPS = 2 * BATCH * PADDED * PADDED * CIN * BASES * COUT
 
 
-def spline_basis(nc, work, x_view, shift, out_view, rows):
+def distance(nc, work, x_view, shift):
     width = x_view.shape[1] * x_view.shape[2]
-    dist = work.tile([P, width], F32)
+    dist = work.tile([P, WIDTH], F32, name="dist")
     nc.scalar.activation(
-        out=dist[:].rearrange("p (w j) -> p w j", j=PACK), in_=x_view, func=ACT.Abs, bias=shift, scale=INV_SPACING
+        out=dist[:, :width].rearrange("p (w j) -> p w j", j=PACK),
+        in_=x_view,
+        func=ACT.Abs,
+        bias=shift,
+        scale=INV_SPACING,
     )
-    outer = work.tile([P, width], F32)
-    nc.vector.tensor_scalar(out=outer[:], in0=dist[:], scalar1=2.0, scalar2=-2.0, op0=ALU.min, op1=ALU.add)
-    inner = work.tile([P, width], F32)
-    nc.vector.tensor_scalar(out=inner[:], in0=dist[:], scalar1=1.0, scalar2=-1.0, op0=ALU.min, op1=ALU.add)
-    outer_sq = work.tile([P, width], F32)
-    nc.scalar.activation(out=outer_sq[:], in_=outer[:], func=ACT.Square, scale=OUTER_ROOT)
-    inner_sq = work.tile([P, width], F32)
-    nc.scalar.activation(out=inner_sq[:], in_=inner[:], func=ACT.Square, scale=INNER_ROOT)
-    outer_cube = work.tile([P, width], F32)
-    nc.vector.tensor_tensor(out=outer_cube[:], in0=outer[:], in1=outer_sq[:], op=ALU.mult)
-    inner_cube = work.tile([P, width], F32)
-    nc.vector.tensor_tensor(out=inner_cube[:], in0=inner[:], in1=inner_sq[:], op=ALU.mult)
-    nc.vector.tensor_tensor(
+    return dist[:, :width]
+
+
+def inner_clamp(nc, work, dist):
+    width = dist.shape[1]
+    inner = work.tile([P, WIDTH], F32, name="inner")
+    nc.vector.tensor_scalar(out=inner[:, :width], in0=dist, scalar1=1.0, scalar2=-1.0, op0=ALU.min, op1=ALU.add)
+    return inner[:, :width]
+
+
+def squares(nc, work, dist, inner):
+    width = dist.shape[1]
+    outer_sq = work.tile([P, WIDTH], F32, name="outer_sq")
+    nc.scalar.activation(
+        out=outer_sq[:, :width], in_=dist, func=ACT.Square, bias=-2.0 * OUTER_ROOT, scale=OUTER_ROOT
+    )
+    inner_sq = work.tile([P, WIDTH], F32, name="inner_sq")
+    nc.scalar.activation(out=inner_sq[:, :width], in_=inner, func=ACT.Square, scale=INNER_ROOT)
+    return outer_sq[:, :width], inner_sq[:, :width]
+
+
+def cubes(nc, work, dist, inner, outer_sq, inner_sq, out_view):
+    width = dist.shape[1]
+    rows = out_view.shape[1]
+    outer_cube = work.tile([P, WIDTH], F32, name="outer_cube")
+    nc.vector.scalar_tensor_tensor(
+        out=outer_cube[:, :width], in0=dist, scalar=-2.0, in1=outer_sq, op0=ALU.add, op1=ALU.mult
+    )
+    inner_cube = work.tile([P, WIDTH], F32, name="inner_cube")
+    nc.vector.tensor_tensor(out=inner_cube[:, :width], in0=inner, in1=inner_sq, op=ALU.mult)
+    nc.vector.scalar_tensor_tensor(
         out=out_view,
-        in0=inner_cube[:].rearrange("p (r c) -> p r c", r=rows),
-        in1=outer_cube[:].rearrange("p (r c) -> p r c", r=rows),
-        op=ALU.subtract,
+        in0=outer_cube[:, :width].rearrange("p (r c) -> p r c", r=rows),
+        scalar=0.0,
+        in1=inner_cube[:, :width].rearrange("p (r c) -> p r c", r=rows),
+        op0=ALU.min,
+        op1=ALU.subtract,
+        reverse1=True,
     )
 
 
@@ -61,24 +88,27 @@ def tile_kanv2d_s_kernel(tc, x, spline_weight, spline_scaler, out):
     with (
         tc.tile_pool(name="keep", bufs=1) as keep,
         tc.tile_pool(name="work", bufs=3) as work,
-        tc.tile_pool(name="results", bufs=4) as results,
+        tc.tile_pool(name="results", bufs=3) as results,
         tc.psum_pool(name="flip", bufs=1) as flip,
-        tc.psum_pool(name="sums", bufs=6) as sums,
+        tc.psum_pool(name="sums", bufs=3) as sums,
+        tc.manual_schedule(),
     ):
-        x_sb = keep.tile([P, BATCH, PACK, SIDE * SIDE], BF16)
+        x_sb = keep.tile([P, BATCH, PACK, SIDE, SIDE], BF16)
 
-        def load_image(n):
+        def load_rows(n, first, last):
             for g in range(BASES):
                 nc.sync.dma_start(
-                    out=x_sb[g:P:BASES, n, :, :], in_=x[n].rearrange("(q j) h w -> q j (h w)", j=PACK)
+                    out=x_sb[g:P:BASES, n, :, first:last, :],
+                    in_=x[n, :, first:last, :].rearrange("(q j) h w -> q j h w", j=PACK),
                 )
 
-        load_image(0)
+        load_rows(0, 0, CHUNK_ROWS - 1)
         weight_sb = keep.tile([P, O_TILES, CIN * BASES], BF16)
         nc.scalar.dma_start(out=weight_sb[:], in_=spline_weight.rearrange("(t p) i g k l -> p t (i g k l)", p=P))
         scaler_sb = keep.tile([P, O_TILES, CIN], BF16)
         nc.scalar.dma_start(out=scaler_sb[:], in_=spline_scaler.rearrange("(t p) i -> p t i", p=P))
-        load_image(1)
+        load_rows(0, CHUNK_ROWS - 1, SIDE)
+        load_rows(1, 0, SIDE)
 
         partition_index = keep.tile([P, 1], I32)
         nc.gpsimd.iota(partition_index[:], pattern=[[0, 1]], base=0, channel_multiplier=1)
@@ -93,7 +123,10 @@ def tile_kanv2d_s_kernel(tc, x, spline_weight, spline_scaler, out):
         zero_x = keep.tile([P, 1, PACK], BF16)
         nc.vector.memset(zero_x[:], 0.0)
         pad_basis = keep.tile([P, 1, PACK], BF16)
-        spline_basis(nc, work, zero_x[:], shift[:], pad_basis[:], 1)
+        pad_dist = distance(nc, work, zero_x[:], shift[:])
+        pad_inner = inner_clamp(nc, work, pad_dist)
+        pad_outer_sq, pad_inner_sq = squares(nc, work, pad_dist, pad_inner)
+        cubes(nc, work, pad_dist, pad_inner, pad_outer_sq, pad_inner_sq, pad_basis[:])
         pad_value = pad_basis[:, :, 0:1]
         for row in (0, PADDED - 1):
             nc.vector.tensor_copy(
@@ -122,48 +155,70 @@ def tile_kanv2d_s_kernel(tc, x, spline_weight, spline_scaler, out):
         for t in range(O_TILES):
             for j in range(PACK):
                 nc.tensor.transpose(flipped[:, t, j, :], scaled[:, t, j, :], identity[:])
-        w_grouped = keep.tile([P, O_TILES, P, PACK], BF16, align_bytes=64)
-        nc.vector.tensor_copy(out=w_grouped[:], in_=flipped[:].rearrange("p t j o -> p t o j"))
         w_codes = keep.tile([P, COUT], U32, align_bytes=64)
         w_scales = keep.tile([P, COUT], U8, align_bytes=64)
-        nc.vector.quantize_mx(
-            out=w_codes[:].bitcast(FP8X4), scales=w_scales[:], in_=w_grouped[:].rearrange("p t o j -> p (t o j)")
-        )
 
-        b_codes = keep.tile([P, BATCH, HALVES, N_TILE], U32, align_bytes=64)
-        b_scales = keep.tile([P, BATCH, HALVES, N_TILE], U8, align_bytes=64)
-        for n in range(BATCH):
-            for h in range(HALVES):
-                pixels = slice(h * HALF_ROWS * SIDE, (h + 1) * HALF_ROWS * SIDE)
-                first_row = 1 + h * HALF_ROWS
-                spline_basis(
+        def finish_weights():
+            w_grouped = keep.tile([P, O_TILES, P, PACK], BF16, align_bytes=64)
+            nc.vector.tensor_copy(out=w_grouped[:], in_=flipped[:].rearrange("p t j o -> p t o j"))
+            nc.vector.quantize_mx(
+                out=w_codes[:].bitcast(FP8X4), scales=w_scales[:], in_=w_grouped[:].rearrange("p t o j -> p (t o j)")
+            )
+
+        b_codes = keep.tile([P, CHUNKS, N_TILE], U32, align_bytes=64)
+        b_scales = keep.tile([P, CHUNKS, N_TILE], U8, align_bytes=64)
+        dist, clamped, squared, acc = {}, {}, {}, {}
+        for step in range(CHUNKS + 3):
+            c = step
+            if c < CHUNKS:
+                n, k = divmod(c, CHUNKS_PER_IMAGE)
+                first = max(1, k * CHUNK_ROWS)
+                last = min(PADDED - 1, (k + 1) * CHUNK_ROWS)
+                dist[c] = distance(
+                    nc, work, x_sb[:, n, :, first - 1 : last - 1, :].rearrange("p j h w -> p (h w) j"), shift[:]
+                )
+            c = step - 1
+            if 0 <= c < CHUNKS:
+                clamped[c] = inner_clamp(nc, work, dist[c])
+                squared[c] = squares(nc, work, dist[c], clamped[c])
+            if step == WEIGHTS_STEP:
+                finish_weights()
+            c = step - 2
+            if 0 <= c < CHUNKS:
+                n, k = divmod(c, CHUNKS_PER_IMAGE)
+                first = max(1, k * CHUNK_ROWS)
+                last = min(PADDED - 1, (k + 1) * CHUNK_ROWS)
+                cubes(
                     nc,
                     work,
-                    x_sb[:, n, :, pixels].rearrange("p j w -> p w j"),
-                    shift[:],
-                    basis[:, n, first_row : first_row + HALF_ROWS, 1 : 1 + SIDE, :].rearrange("p r c j -> p r (c j)"),
-                    HALF_ROWS,
+                    dist[c],
+                    clamped[c],
+                    squared[c][0],
+                    squared[c][1],
+                    basis[:, n, first:last, 1 : 1 + SIDE, :].rearrange("p r c j -> p r (c j)"),
                 )
-                padded_rows = slice(h * HALF_PADDED_ROWS, (h + 1) * HALF_PADDED_ROWS)
                 nc.vector.quantize_mx(
-                    out=b_codes[:, n, h, :].bitcast(FP8X4),
-                    scales=b_scales[:, n, h, :],
-                    in_=basis[:, n, padded_rows, :, :].rearrange("p r c j -> p (r c j)"),
+                    out=b_codes[:, c, :].bitcast(FP8X4),
+                    scales=b_scales[:, c, :],
+                    in_=basis[:, n, k * CHUNK_ROWS : (k + 1) * CHUNK_ROWS, :, :].rearrange("p r c j -> p (r c j)"),
                 )
+                acc[c] = sums.tile([P, O_TILES, N_TILE], F32, name="acc")
                 for t in range(O_TILES):
-                    o_cols = slice(t * P, (t + 1) * P)
-                    acc = sums.tile([P, N_TILE], F32)
                     nc.tensor.matmul_mx(
-                        out=acc[:],
-                        lhsT=w_codes[:, o_cols].bitcast(FP8X4),
-                        lhsT_scale=w_scales[:, o_cols],
-                        rhs=b_codes[:, n, h, :].bitcast(FP8X4),
-                        rhs_scale=b_scales[:, n, h, :],
+                        out=acc[c][:, t, :],
+                        lhsT=w_codes[:, t * P : (t + 1) * P].bitcast(FP8X4),
+                        lhsT_scale=w_scales[:, t * P : (t + 1) * P],
+                        rhs=b_codes[:, c, :].bitcast(FP8X4),
+                        rhs_scale=b_scales[:, c, :],
                         start=True,
                         stop=True,
                     )
-                    result = results.tile([P, N_TILE], F32)
-                    nc.scalar.copy(out=result[:], in_=acc[:])
-                    nc.sync.dma_start(
-                        out=out[n, o_cols, padded_rows, :].rearrange("o y z -> o (y z)"), in_=result[:]
-                    )
+            c = step - 3
+            if 0 <= c < CHUNKS:
+                n, k = divmod(c, CHUNKS_PER_IMAGE)
+                result = results.tile([P, O_TILES, N_TILE], F32)
+                nc.scalar.copy(out=result[:], in_=acc[c][:])
+                nc.sync.dma_start(
+                    out=out[n].rearrange("(t p) y z -> p t (y z)", p=P)[:, :, k * N_TILE : (k + 1) * N_TILE],
+                    in_=result[:],
+                )

@@ -18,11 +18,10 @@ BATCH, CIN, COUT, SIDE = 2, 64, 256, 30
 BASES = 8
 GROUPS = CIN // PACK
 PADDED = SIDE + 2
-CHUNK_ROWS = 8
-CHUNKS_PER_IMAGE = PADDED // CHUNK_ROWS
-CHUNKS = BATCH * CHUNKS_PER_IMAGE
-N_TILE = CHUNK_ROWS * PADDED
-WIDTH = CHUNK_ROWS * SIDE * PACK
+CHUNK_ROWS = (8, 8, 16)
+CHUNKS = BATCH * len(CHUNK_ROWS)
+WIDTH = max(CHUNK_ROWS) * SIDE * PACK
+N_MOST = max(CHUNK_ROWS) * PADDED
 O_TILES = COUT // P
 WEIGHTS_STEP = 1
 INV_SPACING = 2.5
@@ -30,6 +29,14 @@ OUTER_ROOT = math.sqrt(1.0 / 6.0)
 INNER_ROOT = math.sqrt(2.0 / 3.0)
 
 FLOPS = 2 * BATCH * PADDED * PADDED * CIN * BASES * COUT
+
+
+def chunk_shapes():
+    shapes = []
+    for n, sizes in enumerate((CHUNK_ROWS, CHUNK_ROWS[::-1])):
+        for k, size in enumerate(sizes):
+            shapes.append((n, sum(sizes[:k]), size))
+    return shapes
 
 
 def distance(nc, work, x_view, shift):
@@ -90,7 +97,7 @@ def tile_kanv2d_s_kernel(tc, x, spline_weight, spline_scaler, out):
         tc.tile_pool(name="work", bufs=3) as work,
         tc.tile_pool(name="results", bufs=3) as results,
         tc.psum_pool(name="flip", bufs=1) as flip,
-        tc.psum_pool(name="sums", bufs=3) as sums,
+        tc.psum_pool(name="sums", bufs=6) as sums,
         tc.manual_schedule(),
     ):
         x_sb = keep.tile([P, BATCH, PACK, SIDE, SIDE], BF16)
@@ -102,12 +109,12 @@ def tile_kanv2d_s_kernel(tc, x, spline_weight, spline_scaler, out):
                     in_=x[n, :, first:last, :].rearrange("(q j) h w -> q j h w", j=PACK),
                 )
 
-        load_rows(0, 0, CHUNK_ROWS - 1)
+        load_rows(0, 0, CHUNK_ROWS[0] - 1)
         weight_sb = keep.tile([P, O_TILES, CIN * BASES], BF16)
         nc.scalar.dma_start(out=weight_sb[:], in_=spline_weight.rearrange("(t p) i g k l -> p t (i g k l)", p=P))
         scaler_sb = keep.tile([P, O_TILES, CIN], BF16)
         nc.scalar.dma_start(out=scaler_sb[:], in_=spline_scaler.rearrange("(t p) i -> p t i", p=P))
-        load_rows(0, CHUNK_ROWS - 1, SIDE)
+        load_rows(0, CHUNK_ROWS[0] - 1, SIDE)
         load_rows(1, 0, SIDE)
 
         partition_index = keep.tile([P, 1], I32)
@@ -165,15 +172,16 @@ def tile_kanv2d_s_kernel(tc, x, spline_weight, spline_scaler, out):
                 out=w_codes[:].bitcast(FP8X4), scales=w_scales[:], in_=w_grouped[:].rearrange("p t o j -> p (t o j)")
             )
 
-        b_codes = keep.tile([P, CHUNKS, N_TILE], U32, align_bytes=64)
-        b_scales = keep.tile([P, CHUNKS, N_TILE], U8, align_bytes=64)
+        b_codes = keep.tile([P, BATCH, PADDED * PADDED], U32, align_bytes=64)
+        b_scales = keep.tile([P, BATCH, PADDED * PADDED], U8, align_bytes=64)
+        shapes = chunk_shapes()
         dist, clamped, squared, acc = {}, {}, {}, {}
         for step in range(CHUNKS + 3):
             c = step
             if c < CHUNKS:
-                n, k = divmod(c, CHUNKS_PER_IMAGE)
-                first = max(1, k * CHUNK_ROWS)
-                last = min(PADDED - 1, (k + 1) * CHUNK_ROWS)
+                n, row, rows = shapes[c]
+                first = max(1, row)
+                last = min(PADDED - 1, row + rows)
                 dist[c] = distance(
                     nc, work, x_sb[:, n, :, first - 1 : last - 1, :].rearrange("p j h w -> p (h w) j"), shift[:]
                 )
@@ -185,9 +193,10 @@ def tile_kanv2d_s_kernel(tc, x, spline_weight, spline_scaler, out):
                 finish_weights()
             c = step - 2
             if 0 <= c < CHUNKS:
-                n, k = divmod(c, CHUNKS_PER_IMAGE)
-                first = max(1, k * CHUNK_ROWS)
-                last = min(PADDED - 1, (k + 1) * CHUNK_ROWS)
+                n, row, rows = shapes[c]
+                first = max(1, row)
+                last = min(PADDED - 1, row + rows)
+                pixels = slice(row * PADDED, (row + rows) * PADDED)
                 cubes(
                     nc,
                     work,
@@ -198,27 +207,29 @@ def tile_kanv2d_s_kernel(tc, x, spline_weight, spline_scaler, out):
                     basis[:, n, first:last, 1 : 1 + SIDE, :].rearrange("p r c j -> p r (c j)"),
                 )
                 nc.vector.quantize_mx(
-                    out=b_codes[:, c, :].bitcast(FP8X4),
-                    scales=b_scales[:, c, :],
-                    in_=basis[:, n, k * CHUNK_ROWS : (k + 1) * CHUNK_ROWS, :, :].rearrange("p r c j -> p (r c j)"),
+                    out=b_codes[:, n, pixels].bitcast(FP8X4),
+                    scales=b_scales[:, n, pixels],
+                    in_=basis[:, n, row : row + rows, :, :].rearrange("p r c j -> p (r c j)"),
                 )
-                acc[c] = sums.tile([P, O_TILES, N_TILE], F32, name="acc")
                 for t in range(O_TILES):
+                    acc[c, t] = sums.tile([P, N_MOST], F32, name="acc")
                     nc.tensor.matmul_mx(
-                        out=acc[c][:, t, :],
+                        out=acc[c, t][:, : rows * PADDED],
                         lhsT=w_codes[:, t * P : (t + 1) * P].bitcast(FP8X4),
                         lhsT_scale=w_scales[:, t * P : (t + 1) * P],
-                        rhs=b_codes[:, c, :].bitcast(FP8X4),
-                        rhs_scale=b_scales[:, c, :],
+                        rhs=b_codes[:, n, pixels].bitcast(FP8X4),
+                        rhs_scale=b_scales[:, n, pixels],
                         start=True,
                         stop=True,
                     )
             c = step - 3
             if 0 <= c < CHUNKS:
-                n, k = divmod(c, CHUNKS_PER_IMAGE)
-                result = results.tile([P, O_TILES, N_TILE], F32)
-                nc.scalar.copy(out=result[:], in_=acc[c][:])
+                n, row, rows = shapes[c]
+                pixels = slice(row * PADDED, (row + rows) * PADDED)
+                result = results.tile([P, O_TILES, N_MOST], F32)
+                for t in range(O_TILES):
+                    nc.scalar.copy(out=result[:, t, : rows * PADDED], in_=acc[c, t][:, : rows * PADDED])
                 nc.sync.dma_start(
-                    out=out[n].rearrange("(t p) y z -> p t (y z)", p=P)[:, :, k * N_TILE : (k + 1) * N_TILE],
-                    in_=result[:],
+                    out=out[n].rearrange("(t p) y z -> p t (y z)", p=P)[:, :, pixels],
+                    in_=result[:, :, : rows * PADDED],
                 )

@@ -23,7 +23,7 @@ CHUNKS = BATCH * len(CHUNK_ROWS)
 WIDTH = max(CHUNK_ROWS) * SIDE * PACK
 N_MOST = max(CHUNK_ROWS) * PADDED
 O_TILES = COUT // P
-WEIGHTS_STEP = 1
+WEIGHTS_ROUND = -1
 INV_SPACING = 2.5
 OUTER_ROOT = math.sqrt(1.0 / 6.0)
 INNER_ROOT = math.sqrt(2.0 / 3.0)
@@ -52,6 +52,15 @@ def distance(nc, work, x_view, shift):
     return dist[:, :width]
 
 
+def outer_square(nc, work, dist):
+    width = dist.shape[1]
+    outer_sq = work.tile([P, WIDTH], F32, name="outer_sq")
+    nc.scalar.activation(
+        out=outer_sq[:, :width], in_=dist, func=ACT.Square, bias=-2.0 * OUTER_ROOT, scale=OUTER_ROOT
+    )
+    return outer_sq[:, :width]
+
+
 def inner_clamp(nc, work, dist):
     width = dist.shape[1]
     inner = work.tile([P, WIDTH], F32, name="inner")
@@ -59,31 +68,36 @@ def inner_clamp(nc, work, dist):
     return inner[:, :width]
 
 
-def squares(nc, work, dist, inner):
-    width = dist.shape[1]
-    outer_sq = work.tile([P, WIDTH], F32, name="outer_sq")
-    nc.scalar.activation(
-        out=outer_sq[:, :width], in_=dist, func=ACT.Square, bias=-2.0 * OUTER_ROOT, scale=OUTER_ROOT
-    )
+def inner_square(nc, work, inner):
+    width = inner.shape[1]
     inner_sq = work.tile([P, WIDTH], F32, name="inner_sq")
     nc.scalar.activation(out=inner_sq[:, :width], in_=inner, func=ACT.Square, scale=INNER_ROOT)
-    return outer_sq[:, :width], inner_sq[:, :width]
+    return inner_sq[:, :width]
 
 
-def cubes(nc, work, dist, inner, outer_sq, inner_sq, out_view):
+def outer_product(nc, work, dist, outer_sq):
     width = dist.shape[1]
-    rows = out_view.shape[1]
     outer_cube = work.tile([P, WIDTH], F32, name="outer_cube")
     nc.vector.scalar_tensor_tensor(
         out=outer_cube[:, :width], in0=dist, scalar=-2.0, in1=outer_sq, op0=ALU.add, op1=ALU.mult
     )
+    return outer_cube[:, :width]
+
+
+def inner_product(nc, work, inner, inner_sq):
+    width = inner.shape[1]
     inner_cube = work.tile([P, WIDTH], F32, name="inner_cube")
     nc.vector.tensor_tensor(out=inner_cube[:, :width], in0=inner, in1=inner_sq, op=ALU.mult)
+    return inner_cube[:, :width]
+
+
+def difference(nc, outer_cube, inner_cube, out_view):
+    rows = out_view.shape[1]
     nc.vector.scalar_tensor_tensor(
         out=out_view,
-        in0=outer_cube[:, :width].rearrange("p (r c) -> p r c", r=rows),
+        in0=outer_cube.rearrange("p (r c) -> p r c", r=rows),
         scalar=0.0,
-        in1=inner_cube[:, :width].rearrange("p (r c) -> p r c", r=rows),
+        in1=inner_cube.rearrange("p (r c) -> p r c", r=rows),
         op0=ALU.min,
         op1=ALU.subtract,
         reverse1=True,
@@ -132,8 +146,9 @@ def tile_kanv2d_s_kernel(tc, x, spline_weight, spline_scaler, out):
         pad_basis = keep.tile([P, 1, PACK], BF16)
         pad_dist = distance(nc, work, zero_x[:], shift[:])
         pad_inner = inner_clamp(nc, work, pad_dist)
-        pad_outer_sq, pad_inner_sq = squares(nc, work, pad_dist, pad_inner)
-        cubes(nc, work, pad_dist, pad_inner, pad_outer_sq, pad_inner_sq, pad_basis[:])
+        pad_outer_cube = outer_product(nc, work, pad_dist, outer_square(nc, work, pad_dist))
+        pad_inner_cube = inner_product(nc, work, pad_inner, inner_square(nc, work, pad_inner))
+        difference(nc, pad_outer_cube, pad_inner_cube, pad_basis[:])
         pad_value = pad_basis[:, :, 0:1]
         for row in (0, PADDED - 1):
             nc.vector.tensor_copy(
@@ -175,46 +190,44 @@ def tile_kanv2d_s_kernel(tc, x, spline_weight, spline_scaler, out):
         b_codes = keep.tile([P, BATCH, PADDED * PADDED], U32, align_bytes=64)
         b_scales = keep.tile([P, BATCH, PADDED * PADDED], U8, align_bytes=64)
         shapes = chunk_shapes()
-        dist, clamped, squared, acc = {}, {}, {}, {}
-        for step in range(CHUNKS + 3):
-            c = step
-            if c < CHUNKS:
-                n, row, rows = shapes[c]
+        chunks = range(CHUNKS)
+        dist, inner, outer_sq, inner_sq, outer_cube, inner_cube, acc = {}, {}, {}, {}, {}, {}, {}
+        for r in range(-2, CHUNKS + 2):
+            if r in chunks:
+                inner_sq[r] = inner_square(nc, work, inner[r])
+            if r + 2 in chunks:
+                n, row, rows = shapes[r + 2]
                 first = max(1, row)
                 last = min(PADDED - 1, row + rows)
-                dist[c] = distance(
+                dist[r + 2] = distance(
                     nc, work, x_sb[:, n, :, first - 1 : last - 1, :].rearrange("p j h w -> p (h w) j"), shift[:]
                 )
-            c = step - 1
-            if 0 <= c < CHUNKS:
-                clamped[c] = inner_clamp(nc, work, dist[c])
-                squared[c] = squares(nc, work, dist[c], clamped[c])
-            if step == WEIGHTS_STEP:
-                finish_weights()
-            c = step - 2
-            if 0 <= c < CHUNKS:
-                n, row, rows = shapes[c]
-                first = max(1, row)
-                last = min(PADDED - 1, row + rows)
+            if r + 1 in chunks:
+                outer_sq[r + 1] = outer_square(nc, work, dist[r + 1])
+            if r - 2 in chunks:
+                n, row, rows = shapes[r - 2]
                 pixels = slice(row * PADDED, (row + rows) * PADDED)
-                cubes(
-                    nc,
-                    work,
-                    dist[c],
-                    clamped[c],
-                    squared[c][0],
-                    squared[c][1],
-                    basis[:, n, first:last, 1 : 1 + SIDE, :].rearrange("p r c j -> p r (c j)"),
+                result = results.tile([P, O_TILES, N_MOST], F32)
+                for t in range(O_TILES):
+                    nc.scalar.copy(out=result[:, t, : rows * PADDED], in_=acc[r - 2, t][:, : rows * PADDED])
+                nc.sync.dma_start(
+                    out=out[n].rearrange("(t p) y z -> p t (y z)", p=P)[:, :, pixels],
+                    in_=result[:, :, : rows * PADDED],
                 )
+            if r in chunks:
+                outer_cube[r] = outer_product(nc, work, dist[r], outer_sq[r])
+            if r - 1 in chunks:
+                n, row, rows = shapes[r - 1]
+                pixels = slice(row * PADDED, (row + rows) * PADDED)
                 nc.vector.quantize_mx(
                     out=b_codes[:, n, pixels].bitcast(FP8X4),
                     scales=b_scales[:, n, pixels],
                     in_=basis[:, n, row : row + rows, :, :].rearrange("p r c j -> p (r c j)"),
                 )
                 for t in range(O_TILES):
-                    acc[c, t] = sums.tile([P, N_MOST], F32, name="acc")
+                    acc[r - 1, t] = sums.tile([P, N_MOST], F32, name="acc")
                     nc.tensor.matmul_mx(
-                        out=acc[c, t][:, : rows * PADDED],
+                        out=acc[r - 1, t][:, : rows * PADDED],
                         lhsT=w_codes[:, t * P : (t + 1) * P].bitcast(FP8X4),
                         lhsT_scale=w_scales[:, t * P : (t + 1) * P],
                         rhs=b_codes[:, n, pixels].bitcast(FP8X4),
@@ -222,14 +235,19 @@ def tile_kanv2d_s_kernel(tc, x, spline_weight, spline_scaler, out):
                         start=True,
                         stop=True,
                     )
-            c = step - 3
-            if 0 <= c < CHUNKS:
-                n, row, rows = shapes[c]
-                pixels = slice(row * PADDED, (row + rows) * PADDED)
-                result = results.tile([P, O_TILES, N_MOST], F32)
-                for t in range(O_TILES):
-                    nc.scalar.copy(out=result[:, t, : rows * PADDED], in_=acc[c, t][:, : rows * PADDED])
-                nc.sync.dma_start(
-                    out=out[n].rearrange("(t p) y z -> p t (y z)", p=P)[:, :, pixels],
-                    in_=result[:, :, : rows * PADDED],
+            if r in chunks:
+                inner_cube[r] = inner_product(nc, work, inner[r], inner_sq[r])
+            if r + 1 in chunks:
+                inner[r + 1] = inner_clamp(nc, work, dist[r + 1])
+            if r == WEIGHTS_ROUND:
+                finish_weights()
+            if r in chunks:
+                n, row, rows = shapes[r]
+                first = max(1, row)
+                last = min(PADDED - 1, row + rows)
+                difference(
+                    nc,
+                    outer_cube[r],
+                    inner_cube[r],
+                    basis[:, n, first:last, 1 : 1 + SIDE, :].rearrange("p r c j -> p r (c j)"),
                 )

@@ -109,27 +109,24 @@ def tile_kanv2d_s_kernel(tc, x, spline_weight, spline_scaler, out):
     with (
         tc.tile_pool(name="keep", bufs=1) as keep,
         tc.tile_pool(name="work", bufs=3) as work,
-        tc.tile_pool(name="results", bufs=3) as results,
+        tc.tile_pool(name="results", bufs=4) as results,
         tc.psum_pool(name="flip", bufs=1) as flip,
         tc.psum_pool(name="sums", bufs=6) as sums,
         tc.manual_schedule(),
     ):
-        x_sb = keep.tile([P, BATCH, PACK, SIDE, SIDE], BF16)
-
-        def load_rows(n, first, last):
-            for g in range(BASES):
-                nc.sync.dma_start(
-                    out=x_sb[g:P:BASES, n, :, first:last, :],
-                    in_=x[n, :, first:last, :].rearrange("(q j) h w -> q j h w", j=PACK),
-                )
-
-        load_rows(0, 0, CHUNK_ROWS[0] - 1)
+        shapes = chunk_shapes()
         weight_sb = keep.tile([P, O_TILES, CIN * BASES], BF16)
         nc.scalar.dma_start(out=weight_sb[:], in_=spline_weight.rearrange("(t p) i g k l -> p t (i g k l)", p=P))
         scaler_sb = keep.tile([P, O_TILES, CIN], BF16)
         nc.scalar.dma_start(out=scaler_sb[:], in_=spline_scaler.rearrange("(t p) i -> p t i", p=P))
-        load_rows(0, CHUNK_ROWS[0] - 1, SIDE)
-        load_rows(1, 0, SIDE)
+        x_sb = keep.tile([P, BATCH, PACK, SIDE, SIDE], BF16)
+        for n, row, rows in shapes:
+            x_rows = slice(max(1, row) - 1, min(PADDED - 1, row + rows) - 1)
+            for g in range(BASES):
+                nc.sync.dma_start(
+                    out=x_sb[g:P:BASES, n, :, x_rows, :],
+                    in_=x[n, :, x_rows, :].rearrange("(q j) h w -> q j h w", j=PACK),
+                )
 
         partition_index = keep.tile([P, 1], I32)
         nc.gpsimd.iota(partition_index[:], pattern=[[0, 1]], base=0, channel_multiplier=1)
@@ -189,12 +186,13 @@ def tile_kanv2d_s_kernel(tc, x, spline_weight, spline_scaler, out):
 
         b_codes = keep.tile([P, BATCH, PADDED * PADDED], U32, align_bytes=64)
         b_scales = keep.tile([P, BATCH, PADDED * PADDED], U8, align_bytes=64)
-        shapes = chunk_shapes()
         chunks = range(CHUNKS)
         dist, inner, outer_sq, inner_sq, outer_cube, inner_cube, acc = {}, {}, {}, {}, {}, {}, {}
         for r in range(-2, CHUNKS + 2):
             if r in chunks:
                 inner_sq[r] = inner_square(nc, work, inner[r])
+            if r + 1 in chunks:
+                outer_sq[r + 1] = outer_square(nc, work, dist[r + 1])
             if r + 2 in chunks:
                 n, row, rows = shapes[r + 2]
                 first = max(1, row)
@@ -202,18 +200,16 @@ def tile_kanv2d_s_kernel(tc, x, spline_weight, spline_scaler, out):
                 dist[r + 2] = distance(
                     nc, work, x_sb[:, n, :, first - 1 : last - 1, :].rearrange("p j h w -> p (h w) j"), shift[:]
                 )
-            if r + 1 in chunks:
-                outer_sq[r + 1] = outer_square(nc, work, dist[r + 1])
             if r - 2 in chunks:
                 n, row, rows = shapes[r - 2]
                 pixels = slice(row * PADDED, (row + rows) * PADDED)
-                result = results.tile([P, O_TILES, N_MOST], F32)
                 for t in range(O_TILES):
-                    nc.scalar.copy(out=result[:, t, : rows * PADDED], in_=acc[r - 2, t][:, : rows * PADDED])
-                nc.sync.dma_start(
-                    out=out[n].rearrange("(t p) y z -> p t (y z)", p=P)[:, :, pixels],
-                    in_=result[:, :, : rows * PADDED],
-                )
+                    result = results.tile([P, N_MOST], F32)
+                    nc.scalar.copy(out=result[:, : rows * PADDED], in_=acc[r - 2, t][:, : rows * PADDED])
+                    nc.sync.dma_start(
+                        out=out[n, t * P : (t + 1) * P, :, :].rearrange("o y z -> o (y z)")[:, pixels],
+                        in_=result[:, : rows * PADDED],
+                    )
             if r in chunks:
                 outer_cube[r] = outer_product(nc, work, dist[r], outer_sq[r])
             if r - 1 in chunks:

@@ -114,22 +114,22 @@ def tile_kanv2d_s_kernel(tc, x, spline_weight, spline_scaler, out):
         tc.psum_pool(name="sums", bufs=6) as sums,
         tc.manual_schedule(),
     ):
-        shapes = chunk_shapes()
-        weight_sb = keep.tile([P, O_TILES, CIN * BASES], BF16)
-        nc.scalar.dma_start(out=weight_sb[:], in_=spline_weight.rearrange("(t p) i g k l -> p t (i g k l)", p=P))
-        scaler_sb = keep.tile([P, O_TILES, CIN], BF16)
-        nc.scalar.dma_start(out=scaler_sb[:], in_=spline_scaler.rearrange("(t p) i -> p t i", p=P))
-        x_sb = keep.tile([P, BATCH, PACK, SIDE, SIDE], BF16)
-        for n, row, rows in shapes:
-            x_rows = slice(max(1, row) - 1, min(PADDED - 1, row + rows) - 1)
-            for g in range(BASES):
-                nc.sync.dma_start(
-                    out=x_sb[g:P:BASES, n, :, x_rows, :],
-                    in_=x[n, :, x_rows, :].rearrange("(q j) h w -> q j h w", j=PACK),
-                )
-
         partition_index = keep.tile([P, 1], I32)
         nc.gpsimd.iota(partition_index[:], pattern=[[0, 1]], base=0, channel_multiplier=1)
+
+        x_sb = keep.tile([P, BATCH, PACK, SIDE, SIDE], BF16)
+        for n in range(BATCH):
+            for x_rows in (slice(0, SIDE // 2), slice(SIDE // 2, SIDE)):
+                for g in range(BASES):
+                    nc.sync.dma_start(
+                        out=x_sb[g:P:BASES, n, :, x_rows, :],
+                        in_=x[n, :, x_rows, :].rearrange("(q j) h w -> q j h w", j=PACK),
+                    )
+        weight_sb = keep.tile([P, O_TILES, CIN * BASES], BF16)
+        nc.gpsimd.dma_start(out=weight_sb[:], in_=spline_weight.rearrange("(t p) i g k l -> p t (i g k l)", p=P))
+        scaler_sb = keep.tile([P, O_TILES, CIN], BF16)
+        nc.gpsimd.dma_start(out=scaler_sb[:], in_=spline_scaler.rearrange("(t p) i -> p t i", p=P))
+
         basis_index = keep.tile([P, 1], I32)
         nc.vector.tensor_single_scalar(out=basis_index[:], in_=partition_index[:], scalar=BASES - 1, op=ALU.bitwise_and)
         shift = keep.tile([P, 1], F32)
@@ -186,6 +186,7 @@ def tile_kanv2d_s_kernel(tc, x, spline_weight, spline_scaler, out):
 
         b_codes = keep.tile([P, BATCH, PADDED * PADDED], U32, align_bytes=64)
         b_scales = keep.tile([P, BATCH, PADDED * PADDED], U8, align_bytes=64)
+        shapes = chunk_shapes()
         chunks = range(CHUNKS)
         dist, inner, outer_sq, inner_sq, outer_cube, inner_cube, acc = {}, {}, {}, {}, {}, {}, {}
         for r in range(-2, CHUNKS + 2):

@@ -117,14 +117,15 @@ def tile_kanv2d_s_kernel(tc, x, spline_weight, spline_scaler, out):
         partition_index = keep.tile([P, 1], I32)
         nc.gpsimd.iota(partition_index[:], pattern=[[0, 1]], base=0, channel_multiplier=1)
 
+        shapes = chunk_shapes()
         x_sb = keep.tile([P, BATCH, PACK, SIDE, SIDE], BF16)
-        for n in range(BATCH):
-            for x_rows in (slice(0, SIDE // 2), slice(SIDE // 2, SIDE)):
-                for g in range(BASES):
-                    nc.sync.dma_start(
-                        out=x_sb[g:P:BASES, n, :, x_rows, :],
-                        in_=x[n, :, x_rows, :].rearrange("(q j) h w -> q j h w", j=PACK),
-                    )
+        for n, row, rows in shapes:
+            x_rows = slice(max(1, row) - 1, min(PADDED - 1, row + rows) - 1)
+            for g in range(BASES):
+                nc.sync.dma_start(
+                    out=x_sb[g:P:BASES, n, :, x_rows, :],
+                    in_=x[n, :, x_rows, :].rearrange("(q j) h w -> q j h w", j=PACK),
+                )
         weight_sb = keep.tile([P, O_TILES, CIN * BASES], BF16)
         nc.gpsimd.dma_start(out=weight_sb[:], in_=spline_weight.rearrange("(t p) i g k l -> p t (i g k l)", p=P))
         scaler_sb = keep.tile([P, O_TILES, CIN], BF16)
@@ -157,27 +158,29 @@ def tile_kanv2d_s_kernel(tc, x, spline_weight, spline_scaler, out):
                 out=basis[:, :, :, col, :], in_=pad_value.unsqueeze(3).to_broadcast([P, BATCH, PADDED, PACK])
             )
 
-        scaled = keep.tile([P, O_TILES, PACK, P], BF16)
-        for t in range(O_TILES):
-            nc.vector.tensor_tensor(
-                out=scaled[:, t, :, :].rearrange("p j (q g) -> p j q g", g=BASES),
-                in0=weight_sb[:, t, :].rearrange("p (q j g) -> p j q g", j=PACK, g=BASES),
-                in1=scaler_sb[:, t, :]
-                .rearrange("p (q j) -> p j q", j=PACK)
-                .unsqueeze(3)
-                .to_broadcast([P, PACK, GROUPS, BASES]),
-                op=ALU.mult,
-            )
         identity = keep.tile([P, P], BF16)
         make_identity(nc, identity[:])
         flipped = flip.tile([P, O_TILES, PACK, P], BF16)
-        for t in range(O_TILES):
-            for j in range(PACK):
-                nc.tensor.transpose(flipped[:, t, j, :], scaled[:, t, j, :], identity[:])
         w_codes = keep.tile([P, COUT], U32, align_bytes=64)
         w_scales = keep.tile([P, COUT], U8, align_bytes=64)
 
-        def finish_weights():
+        def scale_weights():
+            scaled = keep.tile([P, O_TILES, PACK, P], BF16)
+            for t in range(O_TILES):
+                nc.vector.tensor_tensor(
+                    out=scaled[:, t, :, :].rearrange("p j (q g) -> p j q g", g=BASES),
+                    in0=weight_sb[:, t, :].rearrange("p (q j g) -> p j q g", j=PACK, g=BASES),
+                    in1=scaler_sb[:, t, :]
+                    .rearrange("p (q j) -> p j q", j=PACK)
+                    .unsqueeze(3)
+                    .to_broadcast([P, PACK, GROUPS, BASES]),
+                    op=ALU.mult,
+                )
+            for t in range(O_TILES):
+                for j in range(PACK):
+                    nc.tensor.transpose(flipped[:, t, j, :], scaled[:, t, j, :], identity[:])
+
+        def quantise_weights():
             w_grouped = keep.tile([P, O_TILES, P, PACK], BF16, align_bytes=64)
             nc.vector.tensor_copy(out=w_grouped[:], in_=flipped[:].rearrange("p t j o -> p t o j"))
             nc.vector.quantize_mx(
@@ -186,7 +189,6 @@ def tile_kanv2d_s_kernel(tc, x, spline_weight, spline_scaler, out):
 
         b_codes = keep.tile([P, BATCH, PADDED * PADDED], U32, align_bytes=64)
         b_scales = keep.tile([P, BATCH, PADDED * PADDED], U8, align_bytes=64)
-        shapes = chunk_shapes()
         chunks = range(CHUNKS)
         dist, inner, outer_sq, inner_sq, outer_cube, inner_cube, acc = {}, {}, {}, {}, {}, {}, {}
         for r in range(-2, CHUNKS + 2):
@@ -213,6 +215,8 @@ def tile_kanv2d_s_kernel(tc, x, spline_weight, spline_scaler, out):
                     )
             if r in chunks:
                 outer_cube[r] = outer_product(nc, work, dist[r], outer_sq[r])
+            if r == WEIGHTS_ROUND + 1:
+                quantise_weights()
             if r - 1 in chunks:
                 n, row, rows = shapes[r - 1]
                 pixels = slice(row * PADDED, (row + rows) * PADDED)
@@ -237,7 +241,7 @@ def tile_kanv2d_s_kernel(tc, x, spline_weight, spline_scaler, out):
             if r + 1 in chunks:
                 inner[r + 1] = inner_clamp(nc, work, dist[r + 1])
             if r == WEIGHTS_ROUND:
-                finish_weights()
+                scale_weights()
             if r in chunks:
                 n, row, rows = shapes[r]
                 first = max(1, row)

@@ -61,17 +61,12 @@ def outer_square(nc, work, dist):
     return outer_sq[:, :width]
 
 
-def inner_clamp(nc, work, dist):
+def inner_square(nc, work, dist):
     width = dist.shape[1]
-    inner = work.tile([P, WIDTH], F32, name="inner")
-    nc.vector.tensor_scalar(out=inner[:, :width], in0=dist, scalar1=1.0, scalar2=-1.0, op0=ALU.min, op1=ALU.add)
-    return inner[:, :width]
-
-
-def inner_square(nc, work, inner):
-    width = inner.shape[1]
     inner_sq = work.tile([P, WIDTH], F32, name="inner_sq")
-    nc.scalar.activation(out=inner_sq[:, :width], in_=inner, func=ACT.Square, scale=INNER_ROOT)
+    nc.scalar.activation(
+        out=inner_sq[:, :width], in_=dist, func=ACT.Square, bias=-INNER_ROOT, scale=INNER_ROOT
+    )
     return inner_sq[:, :width]
 
 
@@ -84,10 +79,12 @@ def outer_product(nc, work, dist, outer_sq):
     return outer_cube[:, :width]
 
 
-def inner_product(nc, work, inner, inner_sq):
-    width = inner.shape[1]
+def inner_product(nc, work, dist, inner_sq):
+    width = dist.shape[1]
     inner_cube = work.tile([P, WIDTH], F32, name="inner_cube")
-    nc.vector.tensor_tensor(out=inner_cube[:, :width], in0=inner, in1=inner_sq, op=ALU.mult)
+    nc.vector.scalar_tensor_tensor(
+        out=inner_cube[:, :width], in0=dist, scalar=-1.0, in1=inner_sq, op0=ALU.add, op1=ALU.mult
+    )
     return inner_cube[:, :width]
 
 
@@ -95,13 +92,16 @@ def difference(nc, outer_cube, inner_cube, out_view):
     rows = out_view.shape[1]
     nc.vector.scalar_tensor_tensor(
         out=out_view,
-        in0=outer_cube.rearrange("p (r c) -> p r c", r=rows),
+        in0=inner_cube.rearrange("p (r c) -> p r c", r=rows),
         scalar=0.0,
-        in1=inner_cube.rearrange("p (r c) -> p r c", r=rows),
+        in1=outer_cube.rearrange("p (r c) -> p r c", r=rows),
         op0=ALU.min,
         op1=ALU.subtract,
-        reverse1=True,
     )
+
+
+def clamp(nc, view):
+    nc.vector.tensor_scalar_max(out=view, in0=view, scalar1=0.0)
 
 
 def tile_kanv2d_s_kernel(tc, x, spline_weight, spline_scaler, out):
@@ -143,10 +143,10 @@ def tile_kanv2d_s_kernel(tc, x, spline_weight, spline_scaler, out):
         nc.vector.memset(zero_x[:], 0.0)
         pad_basis = keep.tile([P, 1, PACK], BF16)
         pad_dist = distance(nc, work, zero_x[:], shift[:])
-        pad_inner = inner_clamp(nc, work, pad_dist)
         pad_outer_cube = outer_product(nc, work, pad_dist, outer_square(nc, work, pad_dist))
-        pad_inner_cube = inner_product(nc, work, pad_inner, inner_square(nc, work, pad_inner))
+        pad_inner_cube = inner_product(nc, work, pad_dist, inner_square(nc, work, pad_dist))
         difference(nc, pad_outer_cube, pad_inner_cube, pad_basis[:])
+        clamp(nc, pad_basis[:])
         pad_value = pad_basis[:, :, 0:1]
         for row in (0, PADDED - 1):
             nc.vector.tensor_copy(
@@ -190,12 +190,18 @@ def tile_kanv2d_s_kernel(tc, x, spline_weight, spline_scaler, out):
         b_codes = keep.tile([P, BATCH, PADDED * PADDED], U32, align_bytes=64)
         b_scales = keep.tile([P, BATCH, PADDED * PADDED], U8, align_bytes=64)
         chunks = range(CHUNKS)
-        dist, inner, outer_sq, inner_sq, outer_cube, inner_cube, acc = {}, {}, {}, {}, {}, {}, {}
+        dist, outer_sq, inner_sq, outer_cube, inner_cube, acc = {}, {}, {}, {}, {}, {}
+
+        def interior(c):
+            n, row, rows = shapes[c]
+            first = max(1, row)
+            last = min(PADDED - 1, row + rows)
+            return basis[:, n, first:last, 1 : 1 + SIDE, :].rearrange("p r c j -> p r (c j)")
+
         for r in range(-2, CHUNKS + 2):
-            if r in chunks:
-                inner_sq[r] = inner_square(nc, work, inner[r])
             if r + 1 in chunks:
                 outer_sq[r + 1] = outer_square(nc, work, dist[r + 1])
+                inner_sq[r + 1] = inner_square(nc, work, dist[r + 1])
             if r + 2 in chunks:
                 n, row, rows = shapes[r + 2]
                 first = max(1, row)
@@ -218,6 +224,10 @@ def tile_kanv2d_s_kernel(tc, x, spline_weight, spline_scaler, out):
             if r == WEIGHTS_ROUND + 1:
                 quantise_weights()
             if r - 1 in chunks:
+                clamp(nc, interior(r - 1))
+            if r in chunks:
+                inner_cube[r] = inner_product(nc, work, dist[r], inner_sq[r])
+            if r - 1 in chunks:
                 n, row, rows = shapes[r - 1]
                 pixels = slice(row * PADDED, (row + rows) * PADDED)
                 nc.vector.quantize_mx(
@@ -236,19 +246,7 @@ def tile_kanv2d_s_kernel(tc, x, spline_weight, spline_scaler, out):
                         start=True,
                         stop=True,
                     )
-            if r in chunks:
-                inner_cube[r] = inner_product(nc, work, inner[r], inner_sq[r])
-            if r + 1 in chunks:
-                inner[r + 1] = inner_clamp(nc, work, dist[r + 1])
             if r == WEIGHTS_ROUND:
                 scale_weights()
             if r in chunks:
-                n, row, rows = shapes[r]
-                first = max(1, row)
-                last = min(PADDED - 1, row + rows)
-                difference(
-                    nc,
-                    outer_cube[r],
-                    inner_cube[r],
-                    basis[:, n, first:last, 1 : 1 + SIDE, :].rearrange("p r c j -> p r (c j)"),
-                )
+                difference(nc, outer_cube[r], inner_cube[r], interior(r))

@@ -16,11 +16,14 @@ P = 128
 PACK = 4
 BATCH, CIN, COUT, SIDE = 2, 64, 256, 30
 BASES = 8
-GROUPS = CIN // PACK
+SIDES = 2
+FOLDED = BASES // SIDES
+LANES = PACK // SIDES
+PAIRS = CIN // LANES
 PADDED = SIDE + 2
 CHUNK_ROWS = (8, 8, 16)
 CHUNKS = BATCH * len(CHUNK_ROWS)
-WIDTH = max(CHUNK_ROWS) * SIDE * PACK
+WIDTH = max(CHUNK_ROWS) * SIDE * LANES
 N_MOST = max(CHUNK_ROWS) * PADDED
 O_TILES = COUT // P
 WEIGHTS_ROUND = -1
@@ -39,16 +42,40 @@ def chunk_shapes():
     return shapes
 
 
-def distance(nc, work, x_view, shift):
+def far_distance(nc, work, x_view, shift):
     width = x_view.shape[1] * x_view.shape[2]
-    dist = work.tile([P, WIDTH], F32, name="dist")
+    far = work.tile([P, WIDTH], F32, name="far")
     nc.scalar.activation(
-        out=dist[:, :width].rearrange("p (w j) -> p w j", j=PACK),
+        out=far[:, :width].rearrange("p (w l) -> p w l", l=LANES),
         in_=x_view,
         func=ACT.Abs,
         bias=shift,
         scale=INV_SPACING,
     )
+    return far[:, :width]
+
+
+def signed_offset(nc, deep, x_view, shift):
+    width = x_view.shape[1] * x_view.shape[2]
+    sides = deep.tile([P, SIDES, WIDTH], BF16, name="sides")
+    nc.scalar.activation(
+        out=sides[:, 1, :width].rearrange("p (w l) -> p w l", l=LANES),
+        in_=x_view,
+        func=ACT.Identity,
+        bias=shift,
+        scale=INV_SPACING,
+    )
+    return sides[:, :, :width]
+
+
+def negate(nc, sides):
+    nc.vector.tensor_scalar_mul(out=sides[:, 0, :], in0=sides[:, 1, :], scalar1=-1.0)
+
+
+def near_distance(nc, work, far):
+    width = far.shape[1]
+    dist = work.tile([P, WIDTH], F32, name="dist")
+    nc.scalar.activation(out=dist[:, :width], in_=far, func=ACT.Abs, bias=-2.0, scale=1.0)
     return dist[:, :width]
 
 
@@ -64,9 +91,7 @@ def outer_square(nc, work, dist):
 def inner_square(nc, work, dist):
     width = dist.shape[1]
     inner_sq = work.tile([P, WIDTH], F32, name="inner_sq")
-    nc.scalar.activation(
-        out=inner_sq[:, :width], in_=dist, func=ACT.Square, bias=-INNER_ROOT, scale=INNER_ROOT
-    )
+    nc.scalar.activation(out=inner_sq[:, :width], in_=dist, func=ACT.Square, bias=-INNER_ROOT, scale=INNER_ROOT)
     return inner_sq[:, :width]
 
 
@@ -88,19 +113,29 @@ def inner_product(nc, work, dist, inner_sq):
     return inner_cube[:, :width]
 
 
-def difference(nc, outer_cube, inner_cube, out_view):
-    rows = out_view.shape[1]
+def difference(nc, work, outer_cube, inner_cube):
+    width = outer_cube.shape[1]
+    folded = work.tile([P, WIDTH], BF16, name="folded")
     nc.vector.scalar_tensor_tensor(
+        out=folded[:, :width], in0=inner_cube, scalar=0.0, in1=outer_cube, op0=ALU.min, op1=ALU.subtract
+    )
+    return folded[:, :width]
+
+
+def unfold(nc, folded, sides, out_view):
+    rows, cols = out_view.shape[1], out_view.shape[2]
+    nc.vector.tensor_tensor(
         out=out_view,
-        in0=inner_cube.rearrange("p (r c) -> p r c", r=rows),
-        scalar=0.0,
-        in1=outer_cube.rearrange("p (r c) -> p r c", r=rows),
-        op0=ALU.min,
-        op1=ALU.subtract,
+        in0=folded.rearrange("p (r c l) -> p r c l", r=rows, l=LANES)
+        .unsqueeze(3)
+        .to_broadcast([P, rows, cols, SIDES, LANES]),
+        in1=sides.rearrange("p h (r c l) -> p r c h l", r=rows, l=LANES),
+        op=ALU.min,
     )
 
 
-def clamp(nc, view):
+def clamp(nc, out_view):
+    view = out_view.rearrange("p r c h l -> p r (c h l)")
     nc.vector.tensor_scalar_max(out=view, in0=view, scalar1=0.0)
 
 
@@ -109,6 +144,7 @@ def tile_kanv2d_s_kernel(tc, x, spline_weight, spline_scaler, out):
     with (
         tc.tile_pool(name="keep", bufs=1) as keep,
         tc.tile_pool(name="work", bufs=3) as work,
+        tc.tile_pool(name="deep", bufs=4) as deep,
         tc.tile_pool(name="results", bufs=4) as results,
         tc.psum_pool(name="flip", bufs=1) as flip,
         tc.psum_pool(name="sums", bufs=6) as sums,
@@ -118,44 +154,49 @@ def tile_kanv2d_s_kernel(tc, x, spline_weight, spline_scaler, out):
         nc.gpsimd.iota(partition_index[:], pattern=[[0, 1]], base=0, channel_multiplier=1)
 
         shapes = chunk_shapes()
-        x_sb = keep.tile([P, BATCH, PACK, SIDE, SIDE], BF16)
-        for n, row, rows in shapes:
+        x_sb = []
+        for c, (n, row, rows) in enumerate(shapes):
             x_rows = slice(max(1, row) - 1, min(PADDED - 1, row + rows) - 1)
-            for g in range(BASES):
+            x_chunk = keep.tile([P, LANES, (x_rows.stop - x_rows.start) * SIDE], BF16, name="x%d" % c)
+            x_sb.append(x_chunk)
+            for m in range(FOLDED):
                 nc.sync.dma_start(
-                    out=x_sb[g:P:BASES, n, :, x_rows, :],
-                    in_=x[n, :, x_rows, :].rearrange("(q j) h w -> q j h w", j=PACK),
+                    out=x_chunk[m:P:FOLDED, :, :],
+                    in_=x[n, :, x_rows, :].rearrange("(k l) h w -> k l (h w)", l=LANES),
                 )
         weight_sb = keep.tile([P, O_TILES, CIN * BASES], BF16)
         nc.gpsimd.dma_start(out=weight_sb[:], in_=spline_weight.rearrange("(t p) i g k l -> p t (i g k l)", p=P))
         scaler_sb = keep.tile([P, O_TILES, CIN], BF16)
         nc.gpsimd.dma_start(out=scaler_sb[:], in_=spline_scaler.rearrange("(t p) i -> p t i", p=P))
 
-        basis_index = keep.tile([P, 1], I32)
-        nc.vector.tensor_single_scalar(out=basis_index[:], in_=partition_index[:], scalar=BASES - 1, op=ALU.bitwise_and)
+        pair_index = keep.tile([P, 1], I32)
+        nc.vector.tensor_single_scalar(out=pair_index[:], in_=partition_index[:], scalar=FOLDED - 1, op=ALU.bitwise_and)
         shift = keep.tile([P, 1], F32)
         nc.vector.tensor_scalar(
-            out=shift[:], in0=basis_index[:], scalar1=-1.0, scalar2=(BASES - 1) / 2.0, op0=ALU.mult, op1=ALU.add
+            out=shift[:], in0=pair_index[:], scalar1=-1.0, scalar2=(FOLDED - 1) / 2.0, op0=ALU.mult, op1=ALU.add
         )
 
-        basis = keep.tile([P, BATCH, PADDED, PADDED, PACK], BF16, align_bytes=64)
-        zero_x = keep.tile([P, 1, PACK], BF16)
+        basis = keep.tile([P, BATCH, PADDED, PADDED, SIDES, LANES], BF16, align_bytes=64)
+        zero_x = keep.tile([P, 1, LANES], BF16)
         nc.vector.memset(zero_x[:], 0.0)
-        pad_basis = keep.tile([P, 1, PACK], BF16)
-        pad_dist = distance(nc, work, zero_x[:], shift[:])
+        pad_basis = keep.tile([P, 1, 1, SIDES, LANES], BF16)
+        pad_sides = signed_offset(nc, deep, zero_x[:], shift[:])
+        pad_dist = near_distance(nc, work, far_distance(nc, work, zero_x[:], shift[:]))
+        negate(nc, pad_sides)
         pad_outer_cube = outer_product(nc, work, pad_dist, outer_square(nc, work, pad_dist))
         pad_inner_cube = inner_product(nc, work, pad_dist, inner_square(nc, work, pad_dist))
-        difference(nc, pad_outer_cube, pad_inner_cube, pad_basis[:])
+        unfold(nc, difference(nc, work, pad_outer_cube, pad_inner_cube), pad_sides, pad_basis[:])
         clamp(nc, pad_basis[:])
-        pad_value = pad_basis[:, :, 0:1]
+        pad_word = pad_basis[:].rearrange("p r c h l -> p r c (h l)")
         for row in (0, PADDED - 1):
             nc.vector.tensor_copy(
-                out=basis[:, :, row, :, :].rearrange("p n c j -> p n (c j)"),
-                in_=pad_value.to_broadcast([P, BATCH, PADDED * PACK]),
+                out=basis[:, :, row, :, :, :].rearrange("p n c h l -> p n c (h l)"),
+                in_=pad_word.to_broadcast([P, BATCH, PADDED, PACK]),
             )
         for col in (0, PADDED - 1):
             nc.vector.tensor_copy(
-                out=basis[:, :, :, col, :], in_=pad_value.unsqueeze(3).to_broadcast([P, BATCH, PADDED, PACK])
+                out=basis[:, :, :, col, :, :].rearrange("p n r h l -> p n r (h l)"),
+                in_=pad_word.to_broadcast([P, BATCH, PADDED, PACK]),
             )
 
         identity = keep.tile([P, P], BF16)
@@ -165,20 +206,22 @@ def tile_kanv2d_s_kernel(tc, x, spline_weight, spline_scaler, out):
         w_scales = keep.tile([P, COUT], U8, align_bytes=64)
 
         def scale_weights():
-            scaled = keep.tile([P, O_TILES, PACK, P], BF16)
+            scaled = keep.tile([P, O_TILES, SIDES, LANES, P], BF16)
             for t in range(O_TILES):
-                nc.vector.tensor_tensor(
-                    out=scaled[:, t, :, :].rearrange("p j (q g) -> p j q g", g=BASES),
-                    in0=weight_sb[:, t, :].rearrange("p (q j g) -> p j q g", j=PACK, g=BASES),
-                    in1=scaler_sb[:, t, :]
-                    .rearrange("p (q j) -> p j q", j=PACK)
-                    .unsqueeze(3)
-                    .to_broadcast([P, PACK, GROUPS, BASES]),
-                    op=ALU.mult,
-                )
+                for h in range(SIDES):
+                    nc.vector.tensor_tensor(
+                        out=scaled[:, t, h, :, :].rearrange("p l (k m) -> p l k m", m=FOLDED),
+                        in0=weight_sb[:, t, :].rearrange("p (k l h m) -> p h l k m", l=LANES, h=SIDES, m=FOLDED)[:, h],
+                        in1=scaler_sb[:, t, :]
+                        .rearrange("p (k l) -> p l k", l=LANES)
+                        .unsqueeze(3)
+                        .to_broadcast([P, LANES, PAIRS, FOLDED]),
+                        op=ALU.mult,
+                    )
             for t in range(O_TILES):
-                for j in range(PACK):
-                    nc.tensor.transpose(flipped[:, t, j, :], scaled[:, t, j, :], identity[:])
+                for h in range(SIDES):
+                    for l in range(LANES):
+                        nc.tensor.transpose(flipped[:, t, h * LANES + l, :], scaled[:, t, h, l, :], identity[:])
 
         def quantise_weights():
             w_grouped = keep.tile([P, O_TILES, P, PACK], BF16, align_bytes=64)
@@ -190,25 +233,29 @@ def tile_kanv2d_s_kernel(tc, x, spline_weight, spline_scaler, out):
         b_codes = keep.tile([P, BATCH, PADDED * PADDED], U32, align_bytes=64)
         b_scales = keep.tile([P, BATCH, PADDED * PADDED], U8, align_bytes=64)
         chunks = range(CHUNKS)
-        dist, outer_sq, inner_sq, outer_cube, inner_cube, acc = {}, {}, {}, {}, {}, {}
+        far, sides, dist, outer_sq, inner_sq, outer_cube, inner_cube, folded, acc = {}, {}, {}, {}, {}, {}, {}, {}, {}
+
+        def inner_rows(c):
+            n, row, rows = shapes[c]
+            return n, max(1, row), min(PADDED - 1, row + rows)
+
+        def x_view(c):
+            return x_sb[c][:].rearrange("p l w -> p w l")
 
         def interior(c):
-            n, row, rows = shapes[c]
-            first = max(1, row)
-            last = min(PADDED - 1, row + rows)
-            return basis[:, n, first:last, 1 : 1 + SIDE, :].rearrange("p r c j -> p r (c j)")
+            n, first, last = inner_rows(c)
+            return basis[:, n, first:last, 1 : 1 + SIDE, :, :]
 
         for r in range(-2, CHUNKS + 2):
             if r + 1 in chunks:
                 outer_sq[r + 1] = outer_square(nc, work, dist[r + 1])
+            if r + 2 in chunks:
+                far[r + 2] = far_distance(nc, work, x_view(r + 2), shift[:])
+            if r + 1 in chunks:
                 inner_sq[r + 1] = inner_square(nc, work, dist[r + 1])
             if r + 2 in chunks:
-                n, row, rows = shapes[r + 2]
-                first = max(1, row)
-                last = min(PADDED - 1, row + rows)
-                dist[r + 2] = distance(
-                    nc, work, x_sb[:, n, :, first - 1 : last - 1, :].rearrange("p j h w -> p (h w) j"), shift[:]
-                )
+                sides[r + 2] = signed_offset(nc, deep, x_view(r + 2), shift[:])
+                dist[r + 2] = near_distance(nc, work, far[r + 2])
             if r - 2 in chunks:
                 n, row, rows = shapes[r - 2]
                 pixels = slice(row * PADDED, (row + rows) * PADDED)
@@ -224,16 +271,20 @@ def tile_kanv2d_s_kernel(tc, x, spline_weight, spline_scaler, out):
             if r == WEIGHTS_ROUND + 1:
                 quantise_weights()
             if r - 1 in chunks:
-                clamp(nc, interior(r - 1))
+                unfold(nc, folded[r - 1], sides[r - 1], interior(r - 1))
             if r in chunks:
                 inner_cube[r] = inner_product(nc, work, dist[r], inner_sq[r])
+            if r - 1 in chunks:
+                clamp(nc, interior(r - 1))
+            if r in chunks:
+                folded[r] = difference(nc, work, outer_cube[r], inner_cube[r])
             if r - 1 in chunks:
                 n, row, rows = shapes[r - 1]
                 pixels = slice(row * PADDED, (row + rows) * PADDED)
                 nc.vector.quantize_mx(
                     out=b_codes[:, n, pixels].bitcast(FP8X4),
                     scales=b_scales[:, n, pixels],
-                    in_=basis[:, n, row : row + rows, :, :].rearrange("p r c j -> p (r c j)"),
+                    in_=basis[:, n, row : row + rows, :, :, :].rearrange("p r c h l -> p (r c h l)"),
                 )
                 for t in range(O_TILES):
                     acc[r - 1, t] = sums.tile([P, N_MOST], F32, name="acc")
@@ -246,7 +297,7 @@ def tile_kanv2d_s_kernel(tc, x, spline_weight, spline_scaler, out):
                         start=True,
                         stop=True,
                     )
+            if r + 1 in chunks:
+                negate(nc, sides[r + 1])
             if r == WEIGHTS_ROUND:
                 scale_weights()
-            if r in chunks:
-                difference(nc, outer_cube[r], inner_cube[r], interior(r))

@@ -21,11 +21,13 @@ FOLDED = BASES // SIDES
 LANES = PACK // SIDES
 PAIRS = CIN // LANES
 PADDED = SIDE + 2
-CHUNK_ROWS = (8, 8, 16)
-CHUNKS = BATCH * len(CHUNK_ROWS)
-WIDTH = max(CHUNK_ROWS) * SIDE * LANES
-N_MOST = max(CHUNK_ROWS) * PADDED
+CHUNK_ROWS = ((16, 16), (16, 8, 8))
+CHUNKS = sum(len(sizes) for sizes in CHUNK_ROWS)
+MOST_ROWS = max(max(sizes) for sizes in CHUNK_ROWS)
+WIDTH = MOST_ROWS * SIDE * LANES
+N_MOST = MOST_ROWS * PADDED
 O_TILES = COUT // P
+VECTOR_LEAVES = 0
 WEIGHTS_ROUND = -1
 INV_SPACING = 2.5
 OUTER_ROOT = math.sqrt(1.0 / 6.0)
@@ -36,7 +38,7 @@ FLOPS = 2 * BATCH * PADDED * PADDED * CIN * BASES * COUT
 
 def chunk_shapes():
     shapes = []
-    for n, sizes in enumerate((CHUNK_ROWS, CHUNK_ROWS[::-1])):
+    for n, sizes in enumerate(CHUNK_ROWS):
         for k, size in enumerate(sizes):
             shapes.append((n, sum(sizes[:k]), size))
     return shapes
@@ -145,15 +147,16 @@ def tile_kanv2d_s_kernel(tc, x, spline_weight, spline_scaler, out):
         tc.tile_pool(name="keep", bufs=1) as keep,
         tc.tile_pool(name="work", bufs=3) as work,
         tc.tile_pool(name="deep", bufs=4) as deep,
-        tc.tile_pool(name="results", bufs=4) as results,
-        tc.psum_pool(name="flip", bufs=1) as flip,
-        tc.psum_pool(name="sums", bufs=6) as sums,
+        tc.tile_pool(name="results", bufs=8) as results,
+        tc.psum_pool(name="sums", bufs=8) as sums,
         tc.manual_schedule(),
     ):
         partition_index = keep.tile([P, 1], I32)
         nc.gpsimd.iota(partition_index[:], pattern=[[0, 1]], base=0, channel_multiplier=1)
 
         shapes = chunk_shapes()
+        weight_sb = keep.tile([P, O_TILES, CIN * BASES], BF16)
+        scaler_sb = keep.tile([P, O_TILES, CIN], BF16)
         x_sb = []
         for c, (n, row, rows) in enumerate(shapes):
             x_rows = slice(max(1, row) - 1, min(PADDED - 1, row + rows) - 1)
@@ -164,10 +167,11 @@ def tile_kanv2d_s_kernel(tc, x, spline_weight, spline_scaler, out):
                     out=x_chunk[m:P:FOLDED, :, :],
                     in_=x[n, :, x_rows, :].rearrange("(k l) h w -> k l (h w)", l=LANES),
                 )
-        weight_sb = keep.tile([P, O_TILES, CIN * BASES], BF16)
-        nc.gpsimd.dma_start(out=weight_sb[:], in_=spline_weight.rearrange("(t p) i g k l -> p t (i g k l)", p=P))
-        scaler_sb = keep.tile([P, O_TILES, CIN], BF16)
-        nc.gpsimd.dma_start(out=scaler_sb[:], in_=spline_scaler.rearrange("(t p) i -> p t i", p=P))
+            if c == 0:
+                nc.sync.dma_start(
+                    out=weight_sb[:], in_=spline_weight.rearrange("(t p) i g k l -> p t (i g k l)", p=P)
+                )
+                nc.sync.dma_start(out=scaler_sb[:], in_=spline_scaler.rearrange("(t p) i -> p t i", p=P))
 
         pair_index = keep.tile([P, 1], I32)
         nc.vector.tensor_single_scalar(out=pair_index[:], in_=partition_index[:], scalar=FOLDED - 1, op=ALU.bitwise_and)
@@ -201,7 +205,7 @@ def tile_kanv2d_s_kernel(tc, x, spline_weight, spline_scaler, out):
 
         identity = keep.tile([P, P], BF16)
         make_identity(nc, identity[:])
-        flipped = flip.tile([P, O_TILES, PACK, P], BF16)
+        flipped = sums.tile([P, O_TILES, PACK, P], BF16, name="acc")
         w_codes = keep.tile([P, COUT], U32, align_bytes=64)
         w_scales = keep.tile([P, COUT], U8, align_bytes=64)
 
@@ -246,6 +250,57 @@ def tile_kanv2d_s_kernel(tc, x, spline_weight, spline_scaler, out):
             n, first, last = inner_rows(c)
             return basis[:, n, first:last, 1 : 1 + SIDE, :, :]
 
+        def multiply(c):
+            n, row, rows = shapes[c]
+            width = rows * PADDED
+            pixels = slice(row * PADDED, (row + rows) * PADDED)
+            shared = O_TILES * width <= N_MOST and c != CHUNKS - 1
+            if shared:
+                bank = sums.tile([P, N_MOST], F32, name="acc")
+            for t in range(O_TILES):
+                if shared:
+                    acc[c, t] = bank[:, t * width : (t + 1) * width]
+                else:
+                    alone = sums.tile([P, N_MOST], F32, name="acc")
+                    acc[c, t] = alone[:, :width]
+                nc.tensor.matmul_mx(
+                    out=acc[c, t],
+                    lhsT=w_codes[:, t * P : (t + 1) * P].bitcast(FP8X4),
+                    lhsT_scale=w_scales[:, t * P : (t + 1) * P],
+                    rhs=b_codes[:, n, pixels].bitcast(FP8X4),
+                    rhs_scale=b_scales[:, n, pixels],
+                    start=True,
+                    stop=True,
+                )
+            if shared:
+                acc[c] = bank
+
+        def leave(copy, c, tiles):
+            n, row, rows = shapes[c]
+            width = rows * PADDED
+            pixels = slice(row * PADDED, (row + rows) * PADDED)
+            result = results.tile([P, N_MOST], F32, name="result")
+            if len(tiles) == O_TILES:
+                copy(out=result[:, : O_TILES * width], in_=acc[c][:, : O_TILES * width])
+                nc.sync.dma_start(
+                    out=out[n, :, :, :].rearrange("(t o) y z -> o t (y z)", o=P)[:, :, pixels],
+                    in_=result[:, : O_TILES * width].rearrange("o (t w) -> o t w", t=O_TILES),
+                )
+            else:
+                t = tiles[0]
+                copy(out=result[:, :width], in_=acc[c, t])
+                nc.sync.dma_start(
+                    out=out[n, t * P : (t + 1) * P, :, :].rearrange("o y z -> o (y z)")[:, pixels],
+                    in_=result[:, :width],
+                )
+
+        def leave_all(copy, c):
+            if c in acc:
+                leave(copy, c, list(range(O_TILES)))
+            else:
+                for t in range(O_TILES):
+                    leave(copy, c, [t])
+
         for r in range(-2, CHUNKS + 2):
             if r + 1 in chunks:
                 outer_sq[r + 1] = outer_square(nc, work, dist[r + 1])
@@ -256,16 +311,14 @@ def tile_kanv2d_s_kernel(tc, x, spline_weight, spline_scaler, out):
             if r + 2 in chunks:
                 sides[r + 2] = signed_offset(nc, deep, x_view(r + 2), shift[:])
                 dist[r + 2] = near_distance(nc, work, far[r + 2])
-            if r - 2 in chunks:
-                n, row, rows = shapes[r - 2]
-                pixels = slice(row * PADDED, (row + rows) * PADDED)
-                for t in range(O_TILES):
-                    result = results.tile([P, N_MOST], F32)
-                    nc.scalar.copy(out=result[:, : rows * PADDED], in_=acc[r - 2, t][:, : rows * PADDED])
-                    nc.sync.dma_start(
-                        out=out[n, t * P : (t + 1) * P, :, :].rearrange("o y z -> o (y z)")[:, pixels],
-                        in_=result[:, : rows * PADDED],
-                    )
+            if r == CHUNKS - 1:
+                for c in range(VECTOR_LEAVES, CHUNKS - 2):
+                    leave_all(nc.scalar.copy, c)
+            if r == CHUNKS:
+                leave_all(nc.scalar.copy, CHUNKS - 2)
+            if r == CHUNKS + 1:
+                leave(nc.scalar.copy, CHUNKS - 1, [0])
+                leave(nc.vector.tensor_copy, CHUNKS - 1, [1])
             if r in chunks:
                 outer_cube[r] = outer_product(nc, work, dist[r], outer_sq[r])
             if r == WEIGHTS_ROUND + 1:
@@ -286,18 +339,10 @@ def tile_kanv2d_s_kernel(tc, x, spline_weight, spline_scaler, out):
                     scales=b_scales[:, n, pixels],
                     in_=basis[:, n, row : row + rows, :, :, :].rearrange("p r c h l -> p (r c h l)"),
                 )
-                for t in range(O_TILES):
-                    acc[r - 1, t] = sums.tile([P, N_MOST], F32, name="acc")
-                    nc.tensor.matmul_mx(
-                        out=acc[r - 1, t][:, : rows * PADDED],
-                        lhsT=w_codes[:, t * P : (t + 1) * P].bitcast(FP8X4),
-                        lhsT_scale=w_scales[:, t * P : (t + 1) * P],
-                        rhs=b_codes[:, n, pixels].bitcast(FP8X4),
-                        rhs_scale=b_scales[:, n, pixels],
-                        start=True,
-                        stop=True,
-                    )
+                multiply(r - 1)
             if r + 1 in chunks:
                 negate(nc, sides[r + 1])
+            if r - 2 in range(VECTOR_LEAVES):
+                leave_all(nc.vector.tensor_copy, r - 2)
             if r == WEIGHTS_ROUND:
                 scale_weights()

@@ -151,6 +151,9 @@ def tile_kanv2d_s_kernel(tc, x, spline_weight, spline_scaler, out):
         tc.psum_pool(name="sums", bufs=8) as sums,
         tc.manual_schedule(),
     ):
+        warm = keep.tile([P, 2], F32)
+        nc.gpsimd.memset(warm[:, 0:1], 0.0)
+        nc.scalar.activation(out=warm[:, 1:2], in_=warm[:, 0:1], func=ACT.Abs)
         partition_index = keep.tile([P, 1], I32)
         nc.gpsimd.iota(partition_index[:], pattern=[[0, 1]], base=0, channel_multiplier=1)
 
@@ -175,22 +178,42 @@ def tile_kanv2d_s_kernel(tc, x, spline_weight, spline_scaler, out):
 
         pair_index = keep.tile([P, 1], I32)
         nc.vector.tensor_single_scalar(out=pair_index[:], in_=partition_index[:], scalar=FOLDED - 1, op=ALU.bitwise_and)
-        shift = keep.tile([P, 1], F32)
-        nc.vector.tensor_scalar(
-            out=shift[:], in0=pair_index[:], scalar1=-1.0, scalar2=(FOLDED - 1) / 2.0, op0=ALU.mult, op1=ALU.add
-        )
+        reach = keep.tile([P, SIDES], F32)
+        for h, sign in enumerate((1.0, -1.0)):
+            nc.vector.tensor_scalar(
+                out=reach[:, h : h + 1],
+                in0=pair_index[:],
+                scalar1=sign,
+                scalar2=-sign * (FOLDED - 1) / 2.0,
+                op0=ALU.mult,
+                op1=ALU.add,
+            )
+        shift = reach[:, 1:2]
 
         basis = keep.tile([P, BATCH, PADDED, PADDED, SIDES, LANES], BF16, align_bytes=64)
-        zero_x = keep.tile([P, 1, LANES], BF16)
-        nc.vector.memset(zero_x[:], 0.0)
+        pad_outer = keep.tile([P, SIDES], F32)
+        pad_inner = keep.tile([P, SIDES], F32)
+        pad_outer_sq = keep.tile([P, SIDES], F32)
+        pad_inner_sq = keep.tile([P, SIDES], F32)
+        pad_outer_cube = keep.tile([P, SIDES], F32)
+        pad_inner_cube = keep.tile([P, SIDES], F32)
         pad_basis = keep.tile([P, 1, 1, SIDES, LANES], BF16)
-        pad_sides = signed_offset(nc, deep, zero_x[:], shift[:])
-        pad_dist = near_distance(nc, work, far_distance(nc, work, zero_x[:], shift[:]))
-        negate(nc, pad_sides)
-        pad_outer_cube = outer_product(nc, work, pad_dist, outer_square(nc, work, pad_dist))
-        pad_inner_cube = inner_product(nc, work, pad_dist, inner_square(nc, work, pad_dist))
-        unfold(nc, difference(nc, work, pad_outer_cube, pad_inner_cube), pad_sides, pad_basis[:])
-        clamp(nc, pad_basis[:])
+        nc.vector.tensor_scalar_max(out=pad_outer[:], in0=reach[:], scalar1=0.0)
+        nc.vector.tensor_scalar(out=pad_inner[:], in0=reach[:], scalar1=-1.0, scalar2=0.0, op0=ALU.add, op1=ALU.max)
+        nc.vector.scalar_tensor_tensor(
+            out=pad_outer_sq[:], in0=pad_outer[:], scalar=1.0 / 6.0, in1=pad_outer[:], op0=ALU.mult, op1=ALU.mult
+        )
+        nc.vector.scalar_tensor_tensor(
+            out=pad_inner_sq[:], in0=pad_inner[:], scalar=2.0 / 3.0, in1=pad_inner[:], op0=ALU.mult, op1=ALU.mult
+        )
+        nc.vector.tensor_tensor(out=pad_outer_cube[:], in0=pad_outer_sq[:], in1=pad_outer[:], op=ALU.mult)
+        nc.vector.tensor_tensor(out=pad_inner_cube[:], in0=pad_inner_sq[:], in1=pad_inner[:], op=ALU.mult)
+        nc.vector.tensor_tensor(
+            out=pad_basis[:].rearrange("p r c h l -> p (r c h) l"),
+            in0=pad_outer_cube[:].unsqueeze(2).to_broadcast([P, SIDES, LANES]),
+            in1=pad_inner_cube[:].unsqueeze(2).to_broadcast([P, SIDES, LANES]),
+            op=ALU.subtract,
+        )
         pad_word = pad_basis[:].rearrange("p r c h l -> p r c (h l)")
         for row in (0, PADDED - 1):
             nc.vector.tensor_copy(
@@ -305,12 +328,13 @@ def tile_kanv2d_s_kernel(tc, x, spline_weight, spline_scaler, out):
             if r + 1 in chunks:
                 outer_sq[r + 1] = outer_square(nc, work, dist[r + 1])
             if r + 2 in chunks:
-                far[r + 2] = far_distance(nc, work, x_view(r + 2), shift[:])
+                far[r + 2] = far_distance(nc, work, x_view(r + 2), shift)
             if r + 1 in chunks:
                 inner_sq[r + 1] = inner_square(nc, work, dist[r + 1])
             if r + 2 in chunks:
-                sides[r + 2] = signed_offset(nc, deep, x_view(r + 2), shift[:])
                 dist[r + 2] = near_distance(nc, work, far[r + 2])
+            if r + 1 in chunks:
+                sides[r + 1] = signed_offset(nc, deep, x_view(r + 1), shift)
             if r == CHUNKS - 1:
                 for c in range(VECTOR_LEAVES, CHUNKS - 2):
                     leave_all(nc.scalar.copy, c)
@@ -321,8 +345,6 @@ def tile_kanv2d_s_kernel(tc, x, spline_weight, spline_scaler, out):
                 leave(nc.vector.tensor_copy, CHUNKS - 1, [1])
             if r in chunks:
                 outer_cube[r] = outer_product(nc, work, dist[r], outer_sq[r])
-            if r == WEIGHTS_ROUND + 1:
-                quantise_weights()
             if r - 1 in chunks:
                 unfold(nc, folded[r - 1], sides[r - 1], interior(r - 1))
             if r in chunks:
@@ -340,9 +362,10 @@ def tile_kanv2d_s_kernel(tc, x, spline_weight, spline_scaler, out):
                     in_=basis[:, n, row : row + rows, :, :, :].rearrange("p r c h l -> p (r c h l)"),
                 )
                 multiply(r - 1)
-            if r + 1 in chunks:
-                negate(nc, sides[r + 1])
+            if r in chunks:
+                negate(nc, sides[r])
             if r - 2 in range(VECTOR_LEAVES):
                 leave_all(nc.vector.tensor_copy, r - 2)
             if r == WEIGHTS_ROUND:
                 scale_weights()
+                quantise_weights()

@@ -28,6 +28,7 @@ WIDTH = MOST_ROWS * SIDE * LANES
 N_MOST = MOST_ROWS * PADDED
 O_TILES = COUT // P
 VECTOR_LEAVES = 0
+SCALAR_SIDES = (2, 3, 4)
 WEIGHTS_ROUND = -1
 INV_SPACING = 2.5
 OUTER_ROOT = math.sqrt(1.0 / 6.0)
@@ -72,6 +73,24 @@ def signed_offset(nc, deep, x_view, shift):
 
 def negate(nc, sides):
     nc.vector.tensor_scalar_mul(out=sides[:, 0, :], in0=sides[:, 1, :], scalar1=-1.0)
+
+
+def both_sides(nc, deep, x_view, reach):
+    width = x_view.shape[1] * x_view.shape[2]
+    sides = deep.tile([P, SIDES, WIDTH], BF16, name="sides")
+    for h, sign in enumerate((-1.0, 1.0)):
+        nc.scalar.activation(
+            out=sides[:, h, :width].rearrange("p (w l) -> p w l", l=LANES),
+            in_=x_view,
+            func=ACT.Relu,
+            bias=reach[:, h : h + 1],
+            scale=sign * INV_SPACING,
+        )
+    return sides[:, :, :width]
+
+
+def clamp_folded(nc, folded):
+    nc.vector.tensor_scalar_max(out=folded, in0=folded, scalar1=0.0)
 
 
 def near_distance(nc, work, far):
@@ -333,7 +352,9 @@ def tile_kanv2d_s_kernel(tc, x, spline_weight, spline_scaler, out):
                 inner_sq[r + 1] = inner_square(nc, work, dist[r + 1])
             if r + 2 in chunks:
                 dist[r + 2] = near_distance(nc, work, far[r + 2])
-            if r + 1 in chunks:
+            if r + 1 in chunks and r + 1 in SCALAR_SIDES:
+                sides[r + 1] = both_sides(nc, deep, x_view(r + 1), reach)
+            elif r + 1 in chunks:
                 sides[r + 1] = signed_offset(nc, deep, x_view(r + 1), shift)
             if r == CHUNKS - 1:
                 for c in range(VECTOR_LEAVES, CHUNKS - 2):
@@ -343,13 +364,18 @@ def tile_kanv2d_s_kernel(tc, x, spline_weight, spline_scaler, out):
             if r == CHUNKS + 1:
                 leave(nc.scalar.copy, CHUNKS - 1, [0])
                 leave(nc.vector.tensor_copy, CHUNKS - 1, [1])
+            by_scalar = r - 1 in SCALAR_SIDES
             if r in chunks:
                 outer_cube[r] = outer_product(nc, work, dist[r], outer_sq[r])
-            if r - 1 in chunks:
+            if r - 1 in chunks and by_scalar:
+                clamp_folded(nc, folded[r - 1])
+            elif r - 1 in chunks:
                 unfold(nc, folded[r - 1], sides[r - 1], interior(r - 1))
             if r in chunks:
                 inner_cube[r] = inner_product(nc, work, dist[r], inner_sq[r])
-            if r - 1 in chunks:
+            if r - 1 in chunks and by_scalar:
+                unfold(nc, folded[r - 1], sides[r - 1], interior(r - 1))
+            elif r - 1 in chunks:
                 clamp(nc, interior(r - 1))
             if r in chunks:
                 folded[r] = difference(nc, work, outer_cube[r], inner_cube[r])
@@ -362,7 +388,7 @@ def tile_kanv2d_s_kernel(tc, x, spline_weight, spline_scaler, out):
                     in_=basis[:, n, row : row + rows, :, :, :].rearrange("p r c h l -> p (r c h l)"),
                 )
                 multiply(r - 1)
-            if r in chunks:
+            if r in chunks and r not in SCALAR_SIDES:
                 negate(nc, sides[r])
             if r - 2 in range(VECTOR_LEAVES):
                 leave_all(nc.vector.tensor_copy, r - 2)

@@ -71,6 +71,20 @@ def signed_offset(nc, deep, x_view, shift):
     return sides[:, :, :width]
 
 
+def signed_offset_early(nc, deep, x_view, shift):
+    width = x_view.shape[1] * x_view.shape[2]
+    sides = deep.tile([P, SIDES, WIDTH], BF16, name="sides")
+    nc.gpsimd.tensor_scalar(
+        out=sides[:, 1, :width].rearrange("p (w l) -> p w l", l=LANES),
+        in0=x_view,
+        scalar1=INV_SPACING,
+        scalar2=shift,
+        op0=ALU.mult,
+        op1=ALU.add,
+    )
+    return sides[:, :, :width]
+
+
 def negate(nc, sides):
     nc.vector.tensor_scalar_mul(out=sides[:, 0, :], in0=sides[:, 1, :], scalar1=-1.0)
 
@@ -354,7 +368,7 @@ def tile_kanv2d_s_kernel(tc, x, spline_weight, spline_scaler, out):
                 dist[r + 2] = near_distance(nc, work, far[r + 2])
             if r + 1 in chunks and r + 1 in SCALAR_SIDES:
                 sides[r + 1] = both_sides(nc, deep, x_view(r + 1), reach)
-            elif r + 1 in chunks:
+            elif r + 1 in chunks and r + 1 > 0:
                 sides[r + 1] = signed_offset(nc, deep, x_view(r + 1), shift)
             if r == CHUNKS - 1:
                 for c in range(VECTOR_LEAVES, CHUNKS - 2):
@@ -394,4 +408,7 @@ def tile_kanv2d_s_kernel(tc, x, spline_weight, spline_scaler, out):
                 leave_all(nc.vector.tensor_copy, r - 2)
             if r == WEIGHTS_ROUND:
                 scale_weights()
+                late_shift = keep.tile([P, 1], F32)
+                nc.vector.tensor_copy(out=late_shift[:], in_=shift)
+                sides[0] = signed_offset_early(nc, deep, x_view(0), late_shift[:])
                 quantise_weights()

@@ -357,6 +357,16 @@ def tile_kanv2d_s_kernel(tc, x, spline_weight, spline_scaler, out):
                 for t in range(O_TILES):
                     leave(copy, c, [t])
 
+        def quantise(c):
+            n, row, rows = shapes[c]
+            pixels = slice(row * PADDED, (row + rows) * PADDED)
+            nc.vector.quantize_mx(
+                out=b_codes[:, n, pixels].bitcast(FP8X4),
+                scales=b_scales[:, n, pixels],
+                in_=basis[:, n, row : row + rows, :, :, :].rearrange("p r c h l -> p (r c h l)"),
+            )
+            multiply(c)
+
         for r in range(-2, CHUNKS + 2):
             if r + 1 in chunks:
                 outer_sq[r + 1] = outer_square(nc, work, dist[r + 1])
@@ -378,34 +388,36 @@ def tile_kanv2d_s_kernel(tc, x, spline_weight, spline_scaler, out):
             if r == CHUNKS + 1:
                 leave(nc.scalar.copy, CHUNKS - 1, [0])
                 leave(nc.vector.tensor_copy, CHUNKS - 1, [1])
-            by_scalar = r - 1 in SCALAR_SIDES
-            if r in chunks:
+            last = CHUNKS - 1
+            if r == last:
                 outer_cube[r] = outer_product(nc, work, dist[r], outer_sq[r])
-            if r - 1 in chunks and by_scalar:
-                clamp_folded(nc, folded[r - 1])
-            elif r - 1 in chunks:
-                unfold(nc, folded[r - 1], sides[r - 1], interior(r - 1))
-            if r in chunks:
                 inner_cube[r] = inner_product(nc, work, dist[r], inner_sq[r])
-            if r - 1 in chunks and by_scalar:
-                unfold(nc, folded[r - 1], sides[r - 1], interior(r - 1))
-            elif r - 1 in chunks:
-                clamp(nc, interior(r - 1))
-            if r in chunks:
+                clamp_folded(nc, folded[r - 1])
                 folded[r] = difference(nc, work, outer_cube[r], inner_cube[r])
-            if r - 1 in chunks:
-                n, row, rows = shapes[r - 1]
-                pixels = slice(row * PADDED, (row + rows) * PADDED)
-                nc.vector.quantize_mx(
-                    out=b_codes[:, n, pixels].bitcast(FP8X4),
-                    scales=b_scales[:, n, pixels],
-                    in_=basis[:, n, row : row + rows, :, :, :].rearrange("p r c h l -> p (r c h l)"),
-                )
-                multiply(r - 1)
+                unfold(nc, folded[r - 1], sides[r - 1], interior(r - 1))
+                clamp_folded(nc, folded[r])
+                quantise(r - 1)
+                unfold(nc, folded[r], sides[r], interior(r))
+                quantise(r)
+            by_scalar = r - 1 in SCALAR_SIDES
+            if r in range(last):
+                outer_cube[r] = outer_product(nc, work, dist[r], outer_sq[r])
+            if r - 1 in range(last - 1) and by_scalar:
+                clamp_folded(nc, folded[r - 1])
+            elif r - 1 in range(last - 1):
+                unfold(nc, folded[r - 1], sides[r - 1], interior(r - 1))
+            if r in range(last):
+                inner_cube[r] = inner_product(nc, work, dist[r], inner_sq[r])
+            if r - 1 in range(last - 1) and by_scalar:
+                unfold(nc, folded[r - 1], sides[r - 1], interior(r - 1))
+            elif r - 1 in range(last - 1):
+                clamp(nc, interior(r - 1))
+            if r in range(last):
+                folded[r] = difference(nc, work, outer_cube[r], inner_cube[r])
+            if r - 1 in range(last - 1):
+                quantise(r - 1)
             if r in chunks and r not in SCALAR_SIDES:
                 negate(nc, sides[r])
-            if r - 2 in range(VECTOR_LEAVES):
-                leave_all(nc.vector.tensor_copy, r - 2)
             if r == WEIGHTS_ROUND:
                 scale_weights()
                 late_shift = keep.tile([P, 1], F32)

@@ -29,6 +29,7 @@ N_MOST = MOST_ROWS * PADDED
 O_TILES = COUT // P
 VECTOR_LEAVES = 0
 SCALAR_SIDES = (2, 3, 4)
+WARM_PASSES, WARM_COLUMNS = 4, 256
 WEIGHTS_ROUND = -1
 INV_SPACING = 2.5
 OUTER_ROOT = math.sqrt(1.0 / 6.0)
@@ -393,6 +394,15 @@ def tile_kanv2d_s_kernel(tc, x, spline_weight, spline_scaler, out):
                 outer_cube[r] = outer_product(nc, work, dist[r], outer_sq[r])
                 inner_cube[r] = inner_product(nc, work, dist[r], inner_sq[r])
                 clamp_folded(nc, folded[r - 1])
+                idle_bank = sums.tile([P, N_MOST], F32, name="acc")
+                for k in range(WARM_PASSES):
+                    nc.tensor.matmul(
+                        out=idle_bank[:, :WARM_COLUMNS],
+                        lhsT=identity[:],
+                        rhs=folded[r - 1][:, :WARM_COLUMNS],
+                        start=True,
+                        stop=True,
+                    )
                 folded[r] = difference(nc, work, outer_cube[r], inner_cube[r])
                 unfold(nc, folded[r - 1], sides[r - 1], interior(r - 1))
                 clamp_folded(nc, folded[r])

@@ -21,14 +21,16 @@ FOLDED = BASES // SIDES
 LANES = PACK // SIDES
 PAIRS = CIN // LANES
 PADDED = SIDE + 2
-CHUNK_ROWS = ((16, 16), (16, 8, 8))
+CHUNK_ROWS = ((8, 8, 16), (16, 8, 8))
+LOAD_ROWS = ((16, 16), (32,))
 CHUNKS = sum(len(sizes) for sizes in CHUNK_ROWS)
 MOST_ROWS = max(max(sizes) for sizes in CHUNK_ROWS)
 WIDTH = MOST_ROWS * SIDE * LANES
 N_MOST = MOST_ROWS * PADDED
 O_TILES = COUT // P
 VECTOR_LEAVES = 0
-SCALAR_SIDES = (2, 3, 4)
+BY_VECTOR, BY_SCALAR = range(2)
+SIDES_BY = (BY_VECTOR, BY_VECTOR, BY_VECTOR, BY_SCALAR, BY_SCALAR, BY_SCALAR)
 WARM_PASSES, WARM_COLUMNS = 4, 256
 WEIGHTS_ROUND = -1
 INV_SPACING = 2.5
@@ -38,9 +40,9 @@ INNER_ROOT = math.sqrt(2.0 / 3.0)
 FLOPS = 2 * BATCH * PADDED * PADDED * CIN * BASES * COUT
 
 
-def chunk_shapes():
+def row_ranges(sizes_by_image):
     shapes = []
-    for n, sizes in enumerate(CHUNK_ROWS):
+    for n, sizes in enumerate(sizes_by_image):
         for k, size in enumerate(sizes):
             shapes.append((n, sum(sizes[:k]), size))
     return shapes
@@ -59,35 +61,15 @@ def far_distance(nc, work, x_view, shift):
     return far[:, :width]
 
 
-def signed_offset(nc, deep, x_view, shift):
-    width = x_view.shape[1] * x_view.shape[2]
-    sides = deep.tile([P, SIDES, WIDTH], BF16, name="sides")
-    nc.scalar.activation(
-        out=sides[:, 1, :width].rearrange("p (w l) -> p w l", l=LANES),
-        in_=x_view,
-        func=ACT.Identity,
-        bias=shift,
-        scale=INV_SPACING,
-    )
-    return sides[:, :, :width]
-
-
-def signed_offset_early(nc, deep, x_view, shift):
-    width = x_view.shape[1] * x_view.shape[2]
-    sides = deep.tile([P, SIDES, WIDTH], BF16, name="sides")
-    nc.gpsimd.tensor_scalar(
-        out=sides[:, 1, :width].rearrange("p (w l) -> p w l", l=LANES),
+def mask(nc, sides, x_view, zero, h):
+    nc.vector.tensor_scalar(
+        out=sides[:, h, :].rearrange("p (w l) -> p w l", l=LANES),
         in0=x_view,
-        scalar1=INV_SPACING,
-        scalar2=shift,
-        op0=ALU.mult,
-        op1=ALU.add,
+        scalar1=zero,
+        scalar2=1.0,
+        op0=(ALU.is_lt, ALU.is_ge)[h],
+        op1=ALU.mult,
     )
-    return sides[:, :, :width]
-
-
-def negate(nc, sides):
-    nc.vector.tensor_scalar_mul(out=sides[:, 0, :], in0=sides[:, 1, :], scalar1=-1.0)
 
 
 def both_sides(nc, deep, x_view, reach):
@@ -158,7 +140,7 @@ def difference(nc, work, outer_cube, inner_cube):
     return folded[:, :width]
 
 
-def unfold(nc, folded, sides, out_view):
+def unfold(nc, folded, sides, out_view, op):
     rows, cols = out_view.shape[1], out_view.shape[2]
     nc.vector.tensor_tensor(
         out=out_view,
@@ -166,21 +148,16 @@ def unfold(nc, folded, sides, out_view):
         .unsqueeze(3)
         .to_broadcast([P, rows, cols, SIDES, LANES]),
         in1=sides.rearrange("p h (r c l) -> p r c h l", r=rows, l=LANES),
-        op=ALU.min,
+        op=op,
     )
-
-
-def clamp(nc, out_view):
-    view = out_view.rearrange("p r c h l -> p r (c h l)")
-    nc.vector.tensor_scalar_max(out=view, in0=view, scalar1=0.0)
 
 
 def tile_kanv2d_s_kernel(tc, x, spline_weight, spline_scaler, out):
     nc = tc.nc
     with (
         tc.tile_pool(name="keep", bufs=1) as keep,
-        tc.tile_pool(name="work", bufs=3) as work,
-        tc.tile_pool(name="deep", bufs=4) as deep,
+        tc.tile_pool(name="work", bufs=6) as work,
+        tc.tile_pool(name="deep", bufs=6) as deep,
         tc.tile_pool(name="results", bufs=8) as results,
         tc.psum_pool(name="sums", bufs=8) as sums,
         tc.manual_schedule(),
@@ -191,24 +168,24 @@ def tile_kanv2d_s_kernel(tc, x, spline_weight, spline_scaler, out):
         partition_index = keep.tile([P, 1], I32)
         nc.gpsimd.iota(partition_index[:], pattern=[[0, 1]], base=0, channel_multiplier=1)
 
-        shapes = chunk_shapes()
+        shapes = row_ranges(CHUNK_ROWS)
         weight_sb = keep.tile([P, O_TILES, CIN * BASES], BF16)
         scaler_sb = keep.tile([P, O_TILES, CIN], BF16)
-        x_sb = []
-        for c, (n, row, rows) in enumerate(shapes):
+        x_groups = []
+        for g, (n, row, rows) in enumerate(row_ranges(LOAD_ROWS)):
             x_rows = slice(max(1, row) - 1, min(PADDED - 1, row + rows) - 1)
-            x_chunk = keep.tile([P, LANES, (x_rows.stop - x_rows.start) * SIDE], BF16, name="x%d" % c)
-            x_sb.append(x_chunk)
+            x_group = keep.tile([P, LANES, (x_rows.stop - x_rows.start) * SIDE], BF16, name="x%d" % g)
+            x_groups.append((n, x_rows, x_group))
             for m in range(FOLDED):
                 nc.sync.dma_start(
-                    out=x_chunk[m:P:FOLDED, :, :],
+                    out=x_group[m:P:FOLDED, :, :],
                     in_=x[n, :, x_rows, :].rearrange("(k l) h w -> k l (h w)", l=LANES),
                 )
-            if c == 0:
+            if g == 0:
+                nc.sync.dma_start(out=scaler_sb[:], in_=spline_scaler.rearrange("(t p) i -> p t i", p=P))
                 nc.sync.dma_start(
                     out=weight_sb[:], in_=spline_weight.rearrange("(t p) i g k l -> p t (i g k l)", p=P)
                 )
-                nc.sync.dma_start(out=scaler_sb[:], in_=spline_scaler.rearrange("(t p) i -> p t i", p=P))
 
         pair_index = keep.tile([P, 1], I32)
         nc.vector.tensor_single_scalar(out=pair_index[:], in_=partition_index[:], scalar=FOLDED - 1, op=ALU.bitwise_and)
@@ -223,6 +200,8 @@ def tile_kanv2d_s_kernel(tc, x, spline_weight, spline_scaler, out):
                 op1=ALU.add,
             )
         shift = reach[:, 1:2]
+        zero = keep.tile([P, 1], F32)
+        nc.vector.tensor_scalar_mul(out=zero[:], in0=reach[:, 0:1], scalar1=1.0 / INV_SPACING)
 
         basis = keep.tile([P, BATCH, PADDED, PADDED, SIDES, LANES], BF16, align_bytes=64)
         pad_outer = keep.tile([P, SIDES], F32)
@@ -263,8 +242,24 @@ def tile_kanv2d_s_kernel(tc, x, spline_weight, spline_scaler, out):
         identity = keep.tile([P, P], BF16)
         make_identity(nc, identity[:])
         flipped = sums.tile([P, O_TILES, PACK, P], BF16, name="acc")
+        scaler_wide = keep.tile([P, O_TILES, LANES, P], BF16)
         w_codes = keep.tile([P, COUT], U32, align_bytes=64)
+        w_grouped = keep.tile([P, O_TILES, P, PACK], BF16, align_bytes=64)
         w_scales = keep.tile([P, COUT], U8, align_bytes=64)
+
+        def widen_scaler():
+            for t in range(O_TILES):
+                nc.gpsimd.tensor_scalar(
+                    out=scaler_wide[:, t, :, :].rearrange("p l (k m) -> p l k m", m=FOLDED),
+                    in0=scaler_sb[:, t, :]
+                    .rearrange("p (k l) -> p l k", l=LANES)
+                    .unsqueeze(3)
+                    .to_broadcast([P, LANES, PAIRS, FOLDED]),
+                    scalar1=1.0,
+                    scalar2=0.0,
+                    op0=ALU.mult,
+                    op1=ALU.add,
+                )
 
         def scale_weights():
             scaled = keep.tile([P, O_TILES, SIDES, LANES, P], BF16)
@@ -273,10 +268,7 @@ def tile_kanv2d_s_kernel(tc, x, spline_weight, spline_scaler, out):
                     nc.vector.tensor_tensor(
                         out=scaled[:, t, h, :, :].rearrange("p l (k m) -> p l k m", m=FOLDED),
                         in0=weight_sb[:, t, :].rearrange("p (k l h m) -> p h l k m", l=LANES, h=SIDES, m=FOLDED)[:, h],
-                        in1=scaler_sb[:, t, :]
-                        .rearrange("p (k l) -> p l k", l=LANES)
-                        .unsqueeze(3)
-                        .to_broadcast([P, LANES, PAIRS, FOLDED]),
+                        in1=scaler_wide[:, t, :, :].rearrange("p l (k m) -> p l k m", m=FOLDED),
                         op=ALU.mult,
                     )
             for t in range(O_TILES):
@@ -284,9 +276,10 @@ def tile_kanv2d_s_kernel(tc, x, spline_weight, spline_scaler, out):
                     for l in range(LANES):
                         nc.tensor.transpose(flipped[:, t, h * LANES + l, :], scaled[:, t, h, l, :], identity[:])
 
+        def group_weights():
+            nc.scalar.copy(out=w_grouped[:], in_=flipped[:].rearrange("p t j o -> p t o j"))
+
         def quantise_weights():
-            w_grouped = keep.tile([P, O_TILES, P, PACK], BF16, align_bytes=64)
-            nc.vector.tensor_copy(out=w_grouped[:], in_=flipped[:].rearrange("p t j o -> p t o j"))
             nc.vector.quantize_mx(
                 out=w_codes[:].bitcast(FP8X4), scales=w_scales[:], in_=w_grouped[:].rearrange("p t o j -> p (t o j)")
             )
@@ -301,11 +294,25 @@ def tile_kanv2d_s_kernel(tc, x, spline_weight, spline_scaler, out):
             return n, max(1, row), min(PADDED - 1, row + rows)
 
         def x_view(c):
-            return x_sb[c][:].rearrange("p l w -> p w l")
+            n, first, last = inner_rows(c)
+            for image, x_rows, x_group in x_groups:
+                if n == image and x_rows.start < first <= x_rows.stop:
+                    columns = slice((first - 1 - x_rows.start) * SIDE, (last - 1 - x_rows.start) * SIDE)
+                    return x_group[:, :, columns].rearrange("p l w -> p w l")
 
         def interior(c):
             n, first, last = inner_rows(c)
             return basis[:, n, first:last, 1 : 1 + SIDE, :, :]
+
+        def masks(c):
+            width = x_view(c).shape[1] * LANES
+            both = deep.tile([P, SIDES, WIDTH], BF16, name="sides")
+            sides[c] = both[:, :, :width]
+            for h in range(SIDES):
+                mask(nc, sides[c], x_view(c), zero[:], h)
+
+        def unfold_op(c):
+            return ALU.min if SIDES_BY[c] == BY_SCALAR else ALU.mult
 
         def multiply(c):
             n, row, rows = shapes[c]
@@ -366,21 +373,26 @@ def tile_kanv2d_s_kernel(tc, x, spline_weight, spline_scaler, out):
                 scales=b_scales[:, n, pixels],
                 in_=basis[:, n, row : row + rows, :, :, :].rearrange("p r c h l -> p (r c h l)"),
             )
-            multiply(c)
+            if c > 0:
+                multiply(c)
 
-        for r in range(-2, CHUNKS + 2):
+        far[0] = far_distance(nc, work, x_view(0), shift)
+        far[1] = far_distance(nc, work, x_view(1), shift)
+        dist[0] = near_distance(nc, work, far[0])
+        dist[1] = near_distance(nc, work, far[1])
+        for r in range(-1, CHUNKS + 2):
             if r + 1 in chunks:
                 outer_sq[r + 1] = outer_square(nc, work, dist[r + 1])
-            if r + 2 in chunks:
-                far[r + 2] = far_distance(nc, work, x_view(r + 2), shift)
+            if r + 2 in chunks and r + 2 > 1:
+                dist[r + 2] = near_distance(nc, work, far[r + 2])
             if r + 1 in chunks:
                 inner_sq[r + 1] = inner_square(nc, work, dist[r + 1])
-            if r + 2 in chunks:
-                dist[r + 2] = near_distance(nc, work, far[r + 2])
-            if r + 1 in chunks and r + 1 in SCALAR_SIDES:
+            if r == 0:
+                group_weights()
+            if r + 3 in chunks:
+                far[r + 3] = far_distance(nc, work, x_view(r + 3), shift)
+            if r + 1 in chunks and SIDES_BY[r + 1] == BY_SCALAR:
                 sides[r + 1] = both_sides(nc, deep, x_view(r + 1), reach)
-            elif r + 1 in chunks and r + 1 > 0:
-                sides[r + 1] = signed_offset(nc, deep, x_view(r + 1), shift)
             if r == CHUNKS - 1:
                 for c in range(VECTOR_LEAVES, CHUNKS - 2):
                     leave_all(nc.scalar.copy, c)
@@ -404,33 +416,30 @@ def tile_kanv2d_s_kernel(tc, x, spline_weight, spline_scaler, out):
                         stop=True,
                     )
                 folded[r] = difference(nc, work, outer_cube[r], inner_cube[r])
-                unfold(nc, folded[r - 1], sides[r - 1], interior(r - 1))
+                unfold(nc, folded[r - 1], sides[r - 1], interior(r - 1), unfold_op(r - 1))
                 clamp_folded(nc, folded[r])
                 quantise(r - 1)
-                unfold(nc, folded[r], sides[r], interior(r))
+                unfold(nc, folded[r], sides[r], interior(r), unfold_op(r))
                 quantise(r)
-            by_scalar = r - 1 in SCALAR_SIDES
             if r in range(last):
                 outer_cube[r] = outer_product(nc, work, dist[r], outer_sq[r])
-            if r - 1 in range(last - 1) and by_scalar:
+            if r - 1 in range(last - 1):
                 clamp_folded(nc, folded[r - 1])
-            elif r - 1 in range(last - 1):
-                unfold(nc, folded[r - 1], sides[r - 1], interior(r - 1))
             if r in range(last):
                 inner_cube[r] = inner_product(nc, work, dist[r], inner_sq[r])
-            if r - 1 in range(last - 1) and by_scalar:
-                unfold(nc, folded[r - 1], sides[r - 1], interior(r - 1))
-            elif r - 1 in range(last - 1):
-                clamp(nc, interior(r - 1))
+            if r - 1 in range(last - 1):
+                unfold(nc, folded[r - 1], sides[r - 1], interior(r - 1), unfold_op(r - 1))
             if r in range(last):
                 folded[r] = difference(nc, work, outer_cube[r], inner_cube[r])
             if r - 1 in range(last - 1):
                 quantise(r - 1)
-            if r in chunks and r not in SCALAR_SIDES:
-                negate(nc, sides[r])
             if r == WEIGHTS_ROUND:
+                masks(0)
+                widen_scaler()
                 scale_weights()
-                late_shift = keep.tile([P, 1], F32)
-                nc.vector.tensor_copy(out=late_shift[:], in_=shift)
-                sides[0] = signed_offset_early(nc, deep, x_view(0), late_shift[:])
+                masks(1)
+            if r == 0:
+                masks(2)
+            if r == 1:
                 quantise_weights()
+                multiply(0)

@@ -21,16 +21,16 @@ FOLDED = BASES // SIDES
 LANES = PACK // SIDES
 PAIRS = CIN // LANES
 PADDED = SIDE + 2
-CHUNK_ROWS = ((8, 8, 16), (16, 8, 8))
+CHUNK_ROWS = ((8, 8, 8, 8), (8, 8, 8, 8))
 LOAD_ROWS = ((16, 16), (32,))
+MASK_GROUPS = {(0, 1): -1, (2, 3): 0}
 CHUNKS = sum(len(sizes) for sizes in CHUNK_ROWS)
 MOST_ROWS = max(max(sizes) for sizes in CHUNK_ROWS)
 WIDTH = MOST_ROWS * SIDE * LANES
-N_MOST = MOST_ROWS * PADDED
+N_MOST = 512
 O_TILES = COUT // P
 VECTOR_LEAVES = 0
-BY_VECTOR, BY_SCALAR = range(2)
-SIDES_BY = (BY_VECTOR, BY_VECTOR, BY_VECTOR, BY_SCALAR, BY_SCALAR, BY_SCALAR)
+BY_VECTOR = {c for group in MASK_GROUPS for c in group}
 WARM_PASSES, WARM_COLUMNS = 4, 256
 WEIGHTS_ROUND = -1
 INV_SPACING = 2.5
@@ -294,7 +294,9 @@ def tile_kanv2d_s_kernel(tc, x, spline_weight, spline_scaler, out):
             return n, max(1, row), min(PADDED - 1, row + rows)
 
         def x_view(c):
-            n, first, last = inner_rows(c)
+            return x_rows_view(*inner_rows(c))
+
+        def x_rows_view(n, first, last):
             for image, x_rows, x_group in x_groups:
                 if n == image and x_rows.start < first <= x_rows.stop:
                     columns = slice((first - 1 - x_rows.start) * SIDE, (last - 1 - x_rows.start) * SIDE)
@@ -304,15 +306,20 @@ def tile_kanv2d_s_kernel(tc, x, spline_weight, spline_scaler, out):
             n, first, last = inner_rows(c)
             return basis[:, n, first:last, 1 : 1 + SIDE, :, :]
 
-        def masks(c):
-            width = x_view(c).shape[1] * LANES
-            both = deep.tile([P, SIDES, WIDTH], BF16, name="sides")
-            sides[c] = both[:, :, :width]
+        def masks(group):
+            n, first, last = inner_rows(group[0])[0], inner_rows(group[0])[1], inner_rows(group[-1])[2]
+            width = (last - first) * SIDE * LANES
+            both = keep.tile([P, SIDES, width], BF16, name="masks%d" % group[0])
             for h in range(SIDES):
-                mask(nc, sides[c], x_view(c), zero[:], h)
+                mask(nc, both, x_rows_view(n, first, last), zero[:], h)
+            start = 0
+            for c in group:
+                width = x_view(c).shape[1] * LANES
+                sides[c] = both[:, :, start : start + width]
+                start += width
 
         def unfold_op(c):
-            return ALU.min if SIDES_BY[c] == BY_SCALAR else ALU.mult
+            return ALU.mult if c in BY_VECTOR else ALU.min
 
         def multiply(c):
             n, row, rows = shapes[c]
@@ -391,10 +398,10 @@ def tile_kanv2d_s_kernel(tc, x, spline_weight, spline_scaler, out):
                 group_weights()
             if r + 3 in chunks:
                 far[r + 3] = far_distance(nc, work, x_view(r + 3), shift)
-            if r + 1 in chunks and SIDES_BY[r + 1] == BY_SCALAR:
+            if r + 1 in chunks and r + 1 not in BY_VECTOR:
                 sides[r + 1] = both_sides(nc, deep, x_view(r + 1), reach)
             if r == CHUNKS - 1:
-                for c in range(VECTOR_LEAVES, CHUNKS - 2):
+                for c in range(CHUNKS - 2):
                     leave_all(nc.scalar.copy, c)
             if r == CHUNKS:
                 leave_all(nc.scalar.copy, CHUNKS - 2)
@@ -433,13 +440,12 @@ def tile_kanv2d_s_kernel(tc, x, spline_weight, spline_scaler, out):
                 folded[r] = difference(nc, work, outer_cube[r], inner_cube[r])
             if r - 1 in range(last - 1):
                 quantise(r - 1)
+            for group, at in MASK_GROUPS.items():
+                if at == r:
+                    masks(group)
             if r == WEIGHTS_ROUND:
-                masks(0)
                 widen_scaler()
                 scale_weights()
-                masks(1)
-            if r == 0:
-                masks(2)
             if r == 1:
                 quantise_weights()
                 multiply(0)

@@ -21,18 +21,15 @@ FOLDED = BASES // SIDES
 LANES = PACK // SIDES
 PAIRS = CIN // LANES
 PADDED = SIDE + 2
-CHUNK_ROWS = ((8, 8, 8, 8), (8, 8, 8, 8))
-LOAD_ROWS = ((16, 16), (32,))
-MASK_GROUPS = {(0, 1): -1, (2, 3): 0}
-CHUNKS = sum(len(sizes) for sizes in CHUNK_ROWS)
-MOST_ROWS = max(max(sizes) for sizes in CHUNK_ROWS)
-WIDTH = MOST_ROWS * SIDE * LANES
-N_MOST = 512
+CHUNK_ROWS = 8
+N = CHUNK_ROWS * PADDED
+CHUNKS_PER_IMAGE = PADDED // CHUNK_ROWS
+CHUNKS = BATCH * CHUNKS_PER_IMAGE
+WIDTH = CHUNK_ROWS * SIDE * LANES
 O_TILES = COUT // P
-VECTOR_LEAVES = 0
-BY_VECTOR = {c for group in MASK_GROUPS for c in group}
-WARM_PASSES, WARM_COLUMNS = 4, 256
-WEIGHTS_ROUND = -1
+LOADS = ((0, 0, 2), (0, 2, 2), (1, 0, 4))
+MASK_PAIRS = ((0, 1), (2, 3))
+STORE_LAG = 5
 INV_SPACING = 2.5
 OUTER_ROOT = math.sqrt(1.0 / 6.0)
 INNER_ROOT = math.sqrt(2.0 / 3.0)
@@ -40,12 +37,9 @@ INNER_ROOT = math.sqrt(2.0 / 3.0)
 FLOPS = 2 * BATCH * PADDED * PADDED * CIN * BASES * COUT
 
 
-def row_ranges(sizes_by_image):
-    shapes = []
-    for n, sizes in enumerate(sizes_by_image):
-        for k, size in enumerate(sizes):
-            shapes.append((n, sum(sizes[:k]), size))
-    return shapes
+def rows_of_x(n, chunk, chunks):
+    first = chunk * CHUNK_ROWS
+    return n, slice(max(1, first) - 1, min(PADDED - 1, first + chunks * CHUNK_ROWS) - 1)
 
 
 def far_distance(nc, work, x_view, shift):
@@ -59,35 +53,6 @@ def far_distance(nc, work, x_view, shift):
         scale=INV_SPACING,
     )
     return far[:, :width]
-
-
-def mask(nc, sides, x_view, zero, h):
-    nc.vector.tensor_scalar(
-        out=sides[:, h, :].rearrange("p (w l) -> p w l", l=LANES),
-        in0=x_view,
-        scalar1=zero,
-        scalar2=1.0,
-        op0=(ALU.is_lt, ALU.is_ge)[h],
-        op1=ALU.mult,
-    )
-
-
-def both_sides(nc, deep, x_view, reach):
-    width = x_view.shape[1] * x_view.shape[2]
-    sides = deep.tile([P, SIDES, WIDTH], BF16, name="sides")
-    for h, sign in enumerate((-1.0, 1.0)):
-        nc.scalar.activation(
-            out=sides[:, h, :width].rearrange("p (w l) -> p w l", l=LANES),
-            in_=x_view,
-            func=ACT.Relu,
-            bias=reach[:, h : h + 1],
-            scale=sign * INV_SPACING,
-        )
-    return sides[:, :, :width]
-
-
-def clamp_folded(nc, folded):
-    nc.vector.tensor_scalar_max(out=folded, in0=folded, scalar1=0.0)
 
 
 def near_distance(nc, work, far):
@@ -111,6 +76,37 @@ def inner_square(nc, work, dist):
     inner_sq = work.tile([P, WIDTH], F32, name="inner_sq")
     nc.scalar.activation(out=inner_sq[:, :width], in_=dist, func=ACT.Square, bias=-INNER_ROOT, scale=INNER_ROOT)
     return inner_sq[:, :width]
+
+
+def both_sides(nc, work, x_view, reach):
+    width = x_view.shape[1] * x_view.shape[2]
+    sides = work.tile([P, SIDES, WIDTH], BF16, name="sides")
+    for h, sign in enumerate((-1.0, 1.0)):
+        nc.scalar.activation(
+            out=sides[:, h, :width].rearrange("p (w l) -> p w l", l=LANES),
+            in_=x_view,
+            func=ACT.Relu,
+            bias=reach[:, h : h + 1],
+            scale=sign * INV_SPACING,
+        )
+    return sides[:, :, :width]
+
+
+def upper_mask(nc, both, x_view, zero):
+    nc.vector.tensor_scalar(
+        out=both[:, 1, :].rearrange("p (w l) -> p w l", l=LANES),
+        in0=x_view,
+        scalar1=zero,
+        scalar2=1.0,
+        op0=ALU.is_ge,
+        op1=ALU.mult,
+    )
+
+
+def lower_mask(nc, both):
+    nc.vector.tensor_scalar(
+        out=both[:, 0, :], in0=both[:, 1, :], scalar1=-1.0, scalar2=1.0, op0=ALU.mult, op1=ALU.add
+    )
 
 
 def outer_product(nc, work, dist, outer_sq):
@@ -140,6 +136,10 @@ def difference(nc, work, outer_cube, inner_cube):
     return folded[:, :width]
 
 
+def clamp(nc, folded):
+    nc.vector.tensor_scalar_max(out=folded, in0=folded, scalar1=0.0)
+
+
 def unfold(nc, folded, sides, out_view, op):
     rows, cols = out_view.shape[1], out_view.shape[2]
     nc.vector.tensor_tensor(
@@ -157,7 +157,6 @@ def tile_kanv2d_s_kernel(tc, x, spline_weight, spline_scaler, out):
     with (
         tc.tile_pool(name="keep", bufs=1) as keep,
         tc.tile_pool(name="work", bufs=6) as work,
-        tc.tile_pool(name="deep", bufs=6) as deep,
         tc.tile_pool(name="results", bufs=8) as results,
         tc.psum_pool(name="sums", bufs=8) as sums,
         tc.manual_schedule(),
@@ -168,12 +167,11 @@ def tile_kanv2d_s_kernel(tc, x, spline_weight, spline_scaler, out):
         partition_index = keep.tile([P, 1], I32)
         nc.gpsimd.iota(partition_index[:], pattern=[[0, 1]], base=0, channel_multiplier=1)
 
-        shapes = row_ranges(CHUNK_ROWS)
         weight_sb = keep.tile([P, O_TILES, CIN * BASES], BF16)
         scaler_sb = keep.tile([P, O_TILES, CIN], BF16)
         x_groups = []
-        for g, (n, row, rows) in enumerate(row_ranges(LOAD_ROWS)):
-            x_rows = slice(max(1, row) - 1, min(PADDED - 1, row + rows) - 1)
+        for g, load in enumerate(LOADS):
+            n, x_rows = rows_of_x(*load)
             x_group = keep.tile([P, LANES, (x_rows.stop - x_rows.start) * SIDE], BF16, name="x%d" % g)
             x_groups.append((n, x_rows, x_group))
             for m in range(FOLDED):
@@ -204,47 +202,33 @@ def tile_kanv2d_s_kernel(tc, x, spline_weight, spline_scaler, out):
         nc.vector.tensor_scalar_mul(out=zero[:], in0=reach[:, 0:1], scalar1=1.0 / INV_SPACING)
 
         basis = keep.tile([P, BATCH, PADDED, PADDED, SIDES, LANES], BF16, align_bytes=64)
-        pad_outer = keep.tile([P, SIDES], F32)
-        pad_inner = keep.tile([P, SIDES], F32)
-        pad_outer_sq = keep.tile([P, SIDES], F32)
-        pad_inner_sq = keep.tile([P, SIDES], F32)
-        pad_outer_cube = keep.tile([P, SIDES], F32)
-        pad_inner_cube = keep.tile([P, SIDES], F32)
+        pad_line = keep.tile([P, SIDES], F32)
         pad_basis = keep.tile([P, 1, 1, SIDES, LANES], BF16)
-        nc.vector.tensor_scalar_max(out=pad_outer[:], in0=reach[:], scalar1=0.0)
-        nc.vector.tensor_scalar(out=pad_inner[:], in0=reach[:], scalar1=-1.0, scalar2=0.0, op0=ALU.add, op1=ALU.max)
-        nc.vector.scalar_tensor_tensor(
-            out=pad_outer_sq[:], in0=pad_outer[:], scalar=1.0 / 6.0, in1=pad_outer[:], op0=ALU.mult, op1=ALU.mult
+        nc.vector.tensor_scalar(
+            out=pad_line[:], in0=reach[:], scalar1=11.0 / 24.0, scalar2=-5.0 / 24.0, op0=ALU.mult, op1=ALU.add
         )
-        nc.vector.scalar_tensor_tensor(
-            out=pad_inner_sq[:], in0=pad_inner[:], scalar=2.0 / 3.0, in1=pad_inner[:], op0=ALU.mult, op1=ALU.mult
-        )
-        nc.vector.tensor_tensor(out=pad_outer_cube[:], in0=pad_outer_sq[:], in1=pad_outer[:], op=ALU.mult)
-        nc.vector.tensor_tensor(out=pad_inner_cube[:], in0=pad_inner_sq[:], in1=pad_inner[:], op=ALU.mult)
-        nc.vector.tensor_tensor(
+        nc.vector.tensor_scalar_max(
             out=pad_basis[:].rearrange("p r c h l -> p (r c h) l"),
-            in0=pad_outer_cube[:].unsqueeze(2).to_broadcast([P, SIDES, LANES]),
-            in1=pad_inner_cube[:].unsqueeze(2).to_broadcast([P, SIDES, LANES]),
-            op=ALU.subtract,
+            in0=pad_line[:].unsqueeze(2).to_broadcast([P, SIDES, LANES]),
+            scalar1=0.0,
         )
         pad_word = pad_basis[:].rearrange("p r c h l -> p r c (h l)")
-        for row in (0, PADDED - 1):
+        for n in range(BATCH):
             nc.vector.tensor_copy(
-                out=basis[:, :, row, :, :, :].rearrange("p n c h l -> p n c (h l)"),
-                in_=pad_word.to_broadcast([P, BATCH, PADDED, PACK]),
+                out=basis[:, n, 0 : PADDED : PADDED - 1, :, :, :].rearrange("p r c h l -> p r c (h l)"),
+                in_=pad_word.to_broadcast([P, 2, PADDED, PACK]),
             )
-        for col in (0, PADDED - 1):
             nc.vector.tensor_copy(
-                out=basis[:, :, :, col, :, :].rearrange("p n r h l -> p n r (h l)"),
-                in_=pad_word.to_broadcast([P, BATCH, PADDED, PACK]),
+                out=basis[:, n, 1 : PADDED - 1, 0 : PADDED : PADDED - 1, :, :].rearrange("p r c h l -> p r c (h l)"),
+                in_=pad_word.to_broadcast([P, PADDED - 2, 2, PACK]),
             )
 
         identity = keep.tile([P, P], BF16)
         make_identity(nc, identity[:])
         flipped = sums.tile([P, O_TILES, PACK, P], BF16, name="acc")
         scaler_wide = keep.tile([P, O_TILES, LANES, P], BF16)
-        w_codes = keep.tile([P, COUT], U32, align_bytes=64)
         w_grouped = keep.tile([P, O_TILES, P, PACK], BF16, align_bytes=64)
+        w_codes = keep.tile([P, COUT], U32, align_bytes=64)
         w_scales = keep.tile([P, COUT], U8, align_bytes=64)
 
         def widen_scaler():
@@ -287,55 +271,59 @@ def tile_kanv2d_s_kernel(tc, x, spline_weight, spline_scaler, out):
         b_codes = keep.tile([P, BATCH, PADDED * PADDED], U32, align_bytes=64)
         b_scales = keep.tile([P, BATCH, PADDED * PADDED], U8, align_bytes=64)
         chunks = range(CHUNKS)
-        far, sides, dist, outer_sq, inner_sq, outer_cube, inner_cube, folded, acc = {}, {}, {}, {}, {}, {}, {}, {}, {}
+        far, dist, outer_sq, inner_sq, outer_cube, inner_cube, folded, sides, acc = {}, {}, {}, {}, {}, {}, {}, {}, {}
 
-        def inner_rows(c):
-            n, row, rows = shapes[c]
-            return n, max(1, row), min(PADDED - 1, row + rows)
-
-        def x_view(c):
-            return x_rows_view(*inner_rows(c))
-
-        def x_rows_view(n, first, last):
+        def x_view(c, count):
+            n, wanted = rows_of_x(c // CHUNKS_PER_IMAGE, c % CHUNKS_PER_IMAGE, count)
             for image, x_rows, x_group in x_groups:
-                if n == image and x_rows.start < first <= x_rows.stop:
-                    columns = slice((first - 1 - x_rows.start) * SIDE, (last - 1 - x_rows.start) * SIDE)
+                if n == image and x_rows.start <= wanted.start < x_rows.stop:
+                    columns = slice((wanted.start - x_rows.start) * SIDE, (wanted.stop - x_rows.start) * SIDE)
                     return x_group[:, :, columns].rearrange("p l w -> p w l")
 
+        def columns_of(c):
+            return x_view(c, 1).shape[1] * LANES
+
         def interior(c):
-            n, first, last = inner_rows(c)
-            return basis[:, n, first:last, 1 : 1 + SIDE, :, :]
+            n, x_rows = rows_of_x(c // CHUNKS_PER_IMAGE, c % CHUNKS_PER_IMAGE, 1)
+            return basis[:, n, x_rows.start + 1 : x_rows.stop + 1, 1 : 1 + SIDE, :, :]
 
-        def masks(group):
-            n, first, last = inner_rows(group[0])[0], inner_rows(group[0])[1], inner_rows(group[-1])[2]
-            width = (last - first) * SIDE * LANES
-            both = keep.tile([P, SIDES, width], BF16, name="masks%d" % group[0])
-            for h in range(SIDES):
-                mask(nc, both, x_rows_view(n, first, last), zero[:], h)
-            start = 0
-            for c in group:
-                width = x_view(c).shape[1] * LANES
-                sides[c] = both[:, :, start : start + width]
-                start += width
+        def pixels_of(c):
+            return c // CHUNKS_PER_IMAGE, slice(c % CHUNKS_PER_IMAGE * N, (c % CHUNKS_PER_IMAGE + 1) * N)
 
-        def unfold_op(c):
-            return ALU.mult if c in BY_VECTOR else ALU.min
+        masked = [c for pair in MASK_PAIRS for c in pair]
+        mask_tiles = []
+        for pair in MASK_PAIRS:
+            both = keep.tile([P, SIDES, sum(columns_of(c) for c in pair)], BF16, name="masks%d" % pair[0])
+            mask_tiles.append(both)
+            sides[pair[0]] = both[:, :, : columns_of(pair[0])]
+            sides[pair[1]] = both[:, :, columns_of(pair[0]) :]
+
+        def unfold_rows(c, start, stop):
+            columns = slice(start * SIDE * LANES, stop * SIDE * LANES)
+            op = ALU.mult if c in masked else ALU.min
+            unfold(nc, folded[c][:, columns], sides[c][:, :, columns], interior(c)[:, start:stop], op)
+
+        def unfold_chunk(c):
+            unfold_rows(c, 0, interior(c).shape[1])
+
+        def quantise(c):
+            n, pixels = pixels_of(c)
+            rows = slice(c % CHUNKS_PER_IMAGE * CHUNK_ROWS, (c % CHUNKS_PER_IMAGE + 1) * CHUNK_ROWS)
+            nc.vector.quantize_mx(
+                out=b_codes[:, n, pixels].bitcast(FP8X4),
+                scales=b_scales[:, n, pixels],
+                in_=basis[:, n, rows, :, :, :].rearrange("p r c h l -> p (r c h l)"),
+            )
 
         def multiply(c):
-            n, row, rows = shapes[c]
-            width = rows * PADDED
-            pixels = slice(row * PADDED, (row + rows) * PADDED)
-            shared = O_TILES * width <= N_MOST and c != CHUNKS - 1
-            if shared:
-                bank = sums.tile([P, N_MOST], F32, name="acc")
+            n, pixels = pixels_of(c)
+            bank = sums.tile([P, O_TILES, N], F32, name="acc")
             for t in range(O_TILES):
-                if shared:
-                    acc[c, t] = bank[:, t * width : (t + 1) * width]
-                else:
-                    alone = sums.tile([P, N_MOST], F32, name="acc")
-                    acc[c, t] = alone[:, :width]
+                if c == CHUNKS - 1 and t > 0:
+                    bank = sums.tile([P, O_TILES, N], F32, name="acc")
+                acc[c, t] = bank
                 nc.tensor.matmul_mx(
-                    out=acc[c, t],
+                    out=bank[:, t, :],
                     lhsT=w_codes[:, t * P : (t + 1) * P].bitcast(FP8X4),
                     lhsT_scale=w_scales[:, t * P : (t + 1) * P],
                     rhs=b_codes[:, n, pixels].bitcast(FP8X4),
@@ -343,51 +331,21 @@ def tile_kanv2d_s_kernel(tc, x, spline_weight, spline_scaler, out):
                     start=True,
                     stop=True,
                 )
-            if shared:
-                acc[c] = bank
 
         def leave(copy, c, tiles):
-            n, row, rows = shapes[c]
-            width = rows * PADDED
-            pixels = slice(row * PADDED, (row + rows) * PADDED)
-            result = results.tile([P, N_MOST], F32, name="result")
-            if len(tiles) == O_TILES:
-                copy(out=result[:, : O_TILES * width], in_=acc[c][:, : O_TILES * width])
-                nc.sync.dma_start(
-                    out=out[n, :, :, :].rearrange("(t o) y z -> o t (y z)", o=P)[:, :, pixels],
-                    in_=result[:, : O_TILES * width].rearrange("o (t w) -> o t w", t=O_TILES),
-                )
-            else:
-                t = tiles[0]
-                copy(out=result[:, :width], in_=acc[c, t])
-                nc.sync.dma_start(
-                    out=out[n, t * P : (t + 1) * P, :, :].rearrange("o y z -> o (y z)")[:, pixels],
-                    in_=result[:, :width],
-                )
-
-        def leave_all(copy, c):
-            if c in acc:
-                leave(copy, c, list(range(O_TILES)))
-            else:
-                for t in range(O_TILES):
-                    leave(copy, c, [t])
-
-        def quantise(c):
-            n, row, rows = shapes[c]
-            pixels = slice(row * PADDED, (row + rows) * PADDED)
-            nc.vector.quantize_mx(
-                out=b_codes[:, n, pixels].bitcast(FP8X4),
-                scales=b_scales[:, n, pixels],
-                in_=basis[:, n, row : row + rows, :, :, :].rearrange("p r c h l -> p (r c h l)"),
+            n, pixels = pixels_of(c)
+            result = results.tile([P, O_TILES, N], F32, name="result")
+            copy(out=result[:, tiles, :], in_=acc[c, tiles.start][:, tiles, :])
+            nc.sync.dma_start(
+                out=out[n, :, :, :].rearrange("(t o) y z -> o t (y z)", o=P)[:, tiles, pixels], in_=result[:, tiles, :]
             )
-            if c > 0:
-                multiply(c)
 
-        far[0] = far_distance(nc, work, x_view(0), shift)
-        far[1] = far_distance(nc, work, x_view(1), shift)
+        far[0] = far_distance(nc, work, x_view(0, 1), shift)
+        far[1] = far_distance(nc, work, x_view(1, 1), shift)
         dist[0] = near_distance(nc, work, far[0])
         dist[1] = near_distance(nc, work, far[1])
-        for r in range(-1, CHUNKS + 2):
+        last = CHUNKS - 1
+        for r in range(-1, CHUNKS):
             if r + 1 in chunks:
                 outer_sq[r + 1] = outer_square(nc, work, dist[r + 1])
             if r + 2 in chunks and r + 2 > 1:
@@ -397,55 +355,48 @@ def tile_kanv2d_s_kernel(tc, x, spline_weight, spline_scaler, out):
             if r == 0:
                 group_weights()
             if r + 3 in chunks:
-                far[r + 3] = far_distance(nc, work, x_view(r + 3), shift)
-            if r + 1 in chunks and r + 1 not in BY_VECTOR:
-                sides[r + 1] = both_sides(nc, deep, x_view(r + 1), reach)
-            if r == CHUNKS - 1:
-                for c in range(CHUNKS - 2):
-                    leave_all(nc.scalar.copy, c)
-            if r == CHUNKS:
-                leave_all(nc.scalar.copy, CHUNKS - 2)
-            if r == CHUNKS + 1:
-                leave(nc.scalar.copy, CHUNKS - 1, [0])
-                leave(nc.vector.tensor_copy, CHUNKS - 1, [1])
-            last = CHUNKS - 1
-            if r == last:
-                outer_cube[r] = outer_product(nc, work, dist[r], outer_sq[r])
-                inner_cube[r] = inner_product(nc, work, dist[r], inner_sq[r])
-                clamp_folded(nc, folded[r - 1])
-                idle_bank = sums.tile([P, N_MOST], F32, name="acc")
-                for k in range(WARM_PASSES):
-                    nc.tensor.matmul(
-                        out=idle_bank[:, :WARM_COLUMNS],
-                        lhsT=identity[:],
-                        rhs=folded[r - 1][:, :WARM_COLUMNS],
-                        start=True,
-                        stop=True,
-                    )
-                folded[r] = difference(nc, work, outer_cube[r], inner_cube[r])
-                unfold(nc, folded[r - 1], sides[r - 1], interior(r - 1), unfold_op(r - 1))
-                clamp_folded(nc, folded[r])
-                quantise(r - 1)
-                unfold(nc, folded[r], sides[r], interior(r), unfold_op(r))
-                quantise(r)
-            if r in range(last):
-                outer_cube[r] = outer_product(nc, work, dist[r], outer_sq[r])
-            if r - 1 in range(last - 1):
-                clamp_folded(nc, folded[r - 1])
-            if r in range(last):
-                inner_cube[r] = inner_product(nc, work, dist[r], inner_sq[r])
-            if r - 1 in range(last - 1):
-                unfold(nc, folded[r - 1], sides[r - 1], interior(r - 1), unfold_op(r - 1))
-            if r in range(last):
-                folded[r] = difference(nc, work, outer_cube[r], inner_cube[r])
-            if r - 1 in range(last - 1):
-                quantise(r - 1)
-            for group, at in MASK_GROUPS.items():
-                if at == r:
-                    masks(group)
-            if r == WEIGHTS_ROUND:
+                far[r + 3] = far_distance(nc, work, x_view(r + 3, 1), shift)
+            if r + 1 in chunks and r + 1 not in masked:
+                sides[r + 1] = both_sides(nc, work, x_view(r + 1, 1), reach)
+            if r - STORE_LAG in chunks:
+                leave(nc.scalar.copy, r - STORE_LAG, slice(0, O_TILES))
+            if r == -1:
+                upper_mask(nc, mask_tiles[0], x_view(0, 2), zero[:])
                 widen_scaler()
                 scale_weights()
-            if r == 1:
-                quantise_weights()
-                multiply(0)
+                lower_mask(nc, mask_tiles[0])
+                upper_mask(nc, mask_tiles[1], x_view(2, 2), zero[:])
+            elif r == last:
+                outer_cube[r] = outer_product(nc, work, dist[r], outer_sq[r])
+                clamp(nc, folded[r - 1])
+                inner_cube[r] = inner_product(nc, work, dist[r], inner_sq[r])
+                half = interior(r - 1).shape[1] // 2
+                unfold_rows(r - 1, 0, half)
+                folded[r] = difference(nc, work, outer_cube[r], inner_cube[r])
+                unfold_rows(r - 1, half, interior(r - 1).shape[1])
+                clamp(nc, folded[r])
+                quantise(r - 1)
+                multiply(r - 1)
+                unfold_chunk(r)
+                quantise(r)
+                multiply(r)
+            else:
+                outer_cube[r] = outer_product(nc, work, dist[r], outer_sq[r])
+                if r > 0:
+                    clamp(nc, folded[r - 1])
+                inner_cube[r] = inner_product(nc, work, dist[r], inner_sq[r])
+                if r > 0:
+                    unfold_chunk(r - 1)
+                else:
+                    lower_mask(nc, mask_tiles[1])
+                folded[r] = difference(nc, work, outer_cube[r], inner_cube[r])
+                if r > 0:
+                    quantise(r - 1)
+                if r == 1:
+                    quantise_weights()
+                if r > 0:
+                    multiply(r - 1)
+        for c in range(last - STORE_LAG + 1, last):
+            leave(nc.scalar.copy, c, slice(0, O_TILES))
+        leave(nc.scalar.copy, last, slice(0, 1))
+        leave(nc.vector.tensor_copy, last, slice(1, O_TILES))

@@ -28,8 +28,9 @@ CHUNKS = BATCH * CHUNKS_PER_IMAGE
 WIDTH = CHUNK_ROWS * SIDE * LANES
 O_TILES = COUT // P
 LOADS = ((0, 0, 2), (0, 2, 2), (1, 0, 4))
-MASK_PAIRS = ((0, 1), (2, 3))
-STORE_LAG = 5
+MASK_GROUPS = ((0, 1), (2, 3), (4,))
+WARM_PASSES, WARM_COLUMNS = 4, 256
+STORE_LAG = 6
 INV_SPACING = 2.5
 OUTER_ROOT = math.sqrt(1.0 / 6.0)
 INNER_ROOT = math.sqrt(2.0 / 3.0)
@@ -127,13 +128,10 @@ def inner_product(nc, work, dist, inner_sq):
     return inner_cube[:, :width]
 
 
-def difference(nc, work, outer_cube, inner_cube):
-    width = outer_cube.shape[1]
-    folded = work.tile([P, WIDTH], BF16, name="folded")
+def difference(nc, folded, outer_cube, inner_cube):
     nc.vector.scalar_tensor_tensor(
-        out=folded[:, :width], in0=inner_cube, scalar=0.0, in1=outer_cube, op0=ALU.min, op1=ALU.subtract
+        out=folded, in0=inner_cube, scalar=0.0, in1=outer_cube, op0=ALU.min, op1=ALU.subtract
     )
-    return folded[:, :width]
 
 
 def clamp(nc, folded):
@@ -283,20 +281,30 @@ def tile_kanv2d_s_kernel(tc, x, spline_weight, spline_scaler, out):
         def columns_of(c):
             return x_view(c, 1).shape[1] * LANES
 
+        def make_upper(g):
+            group = MASK_GROUPS[g]
+            upper_mask(nc, mask_tiles[g], x_view(group[0], len(group)), zero[:])
+
+        def make_lower(g):
+            lower_mask(nc, mask_tiles[g])
+
+        def folded_tile(c):
+            whole = work.tile([P, WIDTH], BF16, name="folded")
+            return whole[:, : columns_of(c)]
+
         def interior(c):
             n, x_rows = rows_of_x(c // CHUNKS_PER_IMAGE, c % CHUNKS_PER_IMAGE, 1)
             return basis[:, n, x_rows.start + 1 : x_rows.stop + 1, 1 : 1 + SIDE, :, :]
 
-        def pixels_of(c):
-            return c // CHUNKS_PER_IMAGE, slice(c % CHUNKS_PER_IMAGE * N, (c % CHUNKS_PER_IMAGE + 1) * N)
-
-        masked = [c for pair in MASK_PAIRS for c in pair]
+        masked = [c for group in MASK_GROUPS for c in group]
         mask_tiles = []
-        for pair in MASK_PAIRS:
-            both = keep.tile([P, SIDES, sum(columns_of(c) for c in pair)], BF16, name="masks%d" % pair[0])
+        for group in MASK_GROUPS:
+            both = keep.tile([P, SIDES, x_view(group[0], len(group)).shape[1] * LANES], BF16, name="masks%d" % group[0])
             mask_tiles.append(both)
-            sides[pair[0]] = both[:, :, : columns_of(pair[0])]
-            sides[pair[1]] = both[:, :, columns_of(pair[0]) :]
+            start = 0
+            for c in group:
+                sides[c] = both[:, :, start : start + columns_of(c)]
+                start += columns_of(c)
 
         def unfold_rows(c, start, stop):
             columns = slice(start * SIDE * LANES, stop * SIDE * LANES)
@@ -306,24 +314,23 @@ def tile_kanv2d_s_kernel(tc, x, spline_weight, spline_scaler, out):
         def unfold_chunk(c):
             unfold_rows(c, 0, interior(c).shape[1])
 
-        def quantise(c):
-            n, pixels = pixels_of(c)
-            rows = slice(c % CHUNKS_PER_IMAGE * CHUNK_ROWS, (c % CHUNKS_PER_IMAGE + 1) * CHUNK_ROWS)
+        def quantise(c, row, rows):
+            n, first = c // CHUNKS_PER_IMAGE, c % CHUNKS_PER_IMAGE * CHUNK_ROWS + row
+            pixels = slice(first * PADDED, (first + rows) * PADDED)
             nc.vector.quantize_mx(
                 out=b_codes[:, n, pixels].bitcast(FP8X4),
                 scales=b_scales[:, n, pixels],
-                in_=basis[:, n, rows, :, :, :].rearrange("p r c h l -> p (r c h l)"),
+                in_=basis[:, n, first : first + rows, :, :, :].rearrange("p r c h l -> p (r c h l)"),
             )
 
-        def multiply(c):
-            n, pixels = pixels_of(c)
+        def multiply(c, row, rows):
+            n, first = c // CHUNKS_PER_IMAGE, c % CHUNKS_PER_IMAGE * CHUNK_ROWS + row
+            pixels = slice(first * PADDED, (first + rows) * PADDED)
             bank = sums.tile([P, O_TILES, N], F32, name="acc")
+            acc[c, row] = bank[:].rearrange("p t w -> p (t w)")[:, : O_TILES * rows * PADDED]
             for t in range(O_TILES):
-                if c == CHUNKS - 1 and t > 0:
-                    bank = sums.tile([P, O_TILES, N], F32, name="acc")
-                acc[c, t] = bank
                 nc.tensor.matmul_mx(
-                    out=bank[:, t, :],
+                    out=acc[c, row][:, t * rows * PADDED : (t + 1) * rows * PADDED],
                     lhsT=w_codes[:, t * P : (t + 1) * P].bitcast(FP8X4),
                     lhsT_scale=w_scales[:, t * P : (t + 1) * P],
                     rhs=b_codes[:, n, pixels].bitcast(FP8X4),
@@ -332,71 +339,104 @@ def tile_kanv2d_s_kernel(tc, x, spline_weight, spline_scaler, out):
                     stop=True,
                 )
 
-        def leave(copy, c, tiles):
-            n, pixels = pixels_of(c)
-            result = results.tile([P, O_TILES, N], F32, name="result")
-            copy(out=result[:, tiles, :], in_=acc[c, tiles.start][:, tiles, :])
+        def leave(c, row, rows):
+            n, first = c // CHUNKS_PER_IMAGE, c % CHUNKS_PER_IMAGE * CHUNK_ROWS + row
+            pixels = slice(first * PADDED, (first + rows) * PADDED)
+            result = results.tile([P, O_TILES * N], F32, name="result")
+            width = O_TILES * rows * PADDED
+            nc.scalar.copy(out=result[:, :width], in_=acc[c, row])
             nc.sync.dma_start(
-                out=out[n, :, :, :].rearrange("(t o) y z -> o t (y z)", o=P)[:, tiles, pixels], in_=result[:, tiles, :]
+                out=out[n, :, :, :].rearrange("(t o) y z -> o t (y z)", o=P)[:, :, pixels],
+                in_=result[:, :width].rearrange("o (t w) -> o t w", t=O_TILES),
             )
 
-        far[0] = far_distance(nc, work, x_view(0, 1), shift)
+        def keep_warm(values):
+            idle_bank = sums.tile([P, O_TILES * N], F32, name="acc")
+            for k in range(WARM_PASSES):
+                nc.tensor.matmul(
+                    out=idle_bank[:, :WARM_COLUMNS],
+                    lhsT=identity[:],
+                    rhs=values[:, :WARM_COLUMNS],
+                    start=True,
+                    stop=True,
+                )
+
+        half = CHUNK_ROWS // 2
+        cut = (half - 1) * SIDE
+        xa, xb = x_view(0, 1)[:, :cut], x_view(0, 1)[:, cut:]
+        far_a = far_distance(nc, work, xa, shift)
+        far_b = far_distance(nc, work, xb, shift)
+        dist_a = near_distance(nc, work, far_a)
+        dist_b = near_distance(nc, work, far_b)
+        outer_sq_a = outer_square(nc, work, dist_a)
+        inner_sq_a = inner_square(nc, work, dist_a)
         far[1] = far_distance(nc, work, x_view(1, 1), shift)
-        dist[0] = near_distance(nc, work, far[0])
+        outer_sq_b = outer_square(nc, work, dist_b)
+        inner_sq_b = inner_square(nc, work, dist_b)
         dist[1] = near_distance(nc, work, far[1])
+        far[2] = far_distance(nc, work, x_view(2, 1), shift)
+        make_upper(0)
+        widen_scaler()
+        scale_weights()
+        make_lower(0)
+        make_upper(1)
         last = CHUNKS - 1
-        for r in range(-1, CHUNKS):
+        for r in chunks:
             if r + 1 in chunks:
                 outer_sq[r + 1] = outer_square(nc, work, dist[r + 1])
-            if r + 2 in chunks and r + 2 > 1:
+            if r + 2 in chunks:
                 dist[r + 2] = near_distance(nc, work, far[r + 2])
             if r + 1 in chunks:
                 inner_sq[r + 1] = inner_square(nc, work, dist[r + 1])
-            if r == 0:
+            if r == 1:
                 group_weights()
             if r + 3 in chunks:
                 far[r + 3] = far_distance(nc, work, x_view(r + 3, 1), shift)
             if r + 1 in chunks and r + 1 not in masked:
                 sides[r + 1] = both_sides(nc, work, x_view(r + 1, 1), reach)
             if r - STORE_LAG in chunks:
-                leave(nc.scalar.copy, r - STORE_LAG, slice(0, O_TILES))
-            if r == -1:
-                upper_mask(nc, mask_tiles[0], x_view(0, 2), zero[:])
-                widen_scaler()
-                scale_weights()
-                lower_mask(nc, mask_tiles[0])
-                upper_mask(nc, mask_tiles[1], x_view(2, 2), zero[:])
-            elif r == last:
-                outer_cube[r] = outer_product(nc, work, dist[r], outer_sq[r])
+                leave(r - STORE_LAG, 0, CHUNK_ROWS)
+            folded[r] = folded_tile(r)
+            if r == 0:
+                columns_a, columns_b = folded[0][:, : cut * LANES], folded[0][:, cut * LANES :]
+                outer_cube_a = outer_product(nc, work, dist_a, outer_sq_a)
+                inner_cube_a = inner_product(nc, work, dist_a, inner_sq_a)
+                outer_cube_b = outer_product(nc, work, dist_b, outer_sq_b)
+                difference(nc, columns_a, outer_cube_a, inner_cube_a)
+                inner_cube_b = inner_product(nc, work, dist_b, inner_sq_b)
+                make_lower(1)
+                difference(nc, columns_b, outer_cube_b, inner_cube_b)
+                make_upper(2)
+                clamp(nc, folded[0])
+                continue
+            outer_cube[r] = outer_product(nc, work, dist[r], outer_sq[r])
+            if r > 1:
                 clamp(nc, folded[r - 1])
-                inner_cube[r] = inner_product(nc, work, dist[r], inner_sq[r])
-                half = interior(r - 1).shape[1] // 2
-                unfold_rows(r - 1, 0, half)
-                folded[r] = difference(nc, work, outer_cube[r], inner_cube[r])
-                unfold_rows(r - 1, half, interior(r - 1).shape[1])
-                clamp(nc, folded[r])
-                quantise(r - 1)
-                multiply(r - 1)
-                unfold_chunk(r)
-                quantise(r)
-                multiply(r)
             else:
-                outer_cube[r] = outer_product(nc, work, dist[r], outer_sq[r])
-                if r > 0:
-                    clamp(nc, folded[r - 1])
-                inner_cube[r] = inner_product(nc, work, dist[r], inner_sq[r])
-                if r > 0:
-                    unfold_chunk(r - 1)
-                else:
-                    lower_mask(nc, mask_tiles[1])
-                folded[r] = difference(nc, work, outer_cube[r], inner_cube[r])
-                if r > 0:
-                    quantise(r - 1)
-                if r == 1:
-                    quantise_weights()
-                if r > 0:
-                    multiply(r - 1)
+                make_lower(2)
+                unfold_chunk(0)
+            if r == last:
+                keep_warm(folded[r - 1])
+            inner_cube[r] = inner_product(nc, work, dist[r], inner_sq[r])
+            if r > 1:
+                unfold_chunk(r - 1)
+            else:
+                quantise(0, 0, CHUNK_ROWS)
+            difference(nc, folded[r], outer_cube[r], inner_cube[r])
+            if r > 1:
+                quantise(r - 1, 0, CHUNK_ROWS)
+            if r == 2:
+                quantise_weights()
+                multiply(0, 0, CHUNK_ROWS)
+            if r > 1:
+                multiply(r - 1, 0, CHUNK_ROWS)
+        clamp(nc, folded[last])
+        unfold_rows(last, 0, half)
+        unfold_rows(last, half, interior(last).shape[1])
+        for row in (0, half):
+            quantise(last, row, half)
+            multiply(last, row, half)
         for c in range(last - STORE_LAG + 1, last):
-            leave(nc.scalar.copy, c, slice(0, O_TILES))
-        leave(nc.scalar.copy, last, slice(0, 1))
-        leave(nc.vector.tensor_copy, last, slice(1, O_TILES))
+            leave(c, 0, CHUNK_ROWS)
+        for row in (0, half):
+            leave(last, row, half)

@@ -30,7 +30,7 @@ O_TILES = COUT // P
 LOADS = ((0, 0, 2), (0, 2, 2), (1, 0, 4))
 MASK_GROUPS = ((0, 1), (2, 3), (4,))
 WARM_PASSES, WARM_COLUMNS = 4, 256
-STORE_LAG = 6
+STORES = {4: (0,), 5: (1, 2), 6: (3,), 7: (4, 5), 8: (6,)}
 INV_SPACING = 2.5
 OUTER_ROOT = math.sqrt(1.0 / 6.0)
 INNER_ROOT = math.sqrt(2.0 / 3.0)
@@ -224,39 +224,38 @@ def tile_kanv2d_s_kernel(tc, x, spline_weight, spline_scaler, out):
         identity = keep.tile([P, P], BF16)
         make_identity(nc, identity[:])
         flipped = sums.tile([P, O_TILES, PACK, P], BF16, name="acc")
-        scaler_wide = keep.tile([P, O_TILES, LANES, P], BF16)
+        scaler_wide = keep.tile([P, LANES, O_TILES, P], BF16)
         w_grouped = keep.tile([P, O_TILES, P, PACK], BF16, align_bytes=64)
         w_codes = keep.tile([P, COUT], U32, align_bytes=64)
         w_scales = keep.tile([P, COUT], U8, align_bytes=64)
 
         def widen_scaler():
-            for t in range(O_TILES):
-                nc.gpsimd.tensor_scalar(
-                    out=scaler_wide[:, t, :, :].rearrange("p l (k m) -> p l k m", m=FOLDED),
-                    in0=scaler_sb[:, t, :]
-                    .rearrange("p (k l) -> p l k", l=LANES)
-                    .unsqueeze(3)
-                    .to_broadcast([P, LANES, PAIRS, FOLDED]),
-                    scalar1=1.0,
-                    scalar2=0.0,
-                    op0=ALU.mult,
-                    op1=ALU.add,
-                )
+            nc.gpsimd.tensor_scalar(
+                out=scaler_wide[:].rearrange("p l t (k m) -> p l (t k) m", m=FOLDED),
+                in0=scaler_sb[:]
+                .rearrange("p t (k l) -> p l (t k)", l=LANES)
+                .unsqueeze(3)
+                .to_broadcast([P, LANES, O_TILES * PAIRS, FOLDED]),
+                scalar1=1.0,
+                scalar2=0.0,
+                op0=ALU.mult,
+                op1=ALU.add,
+            )
 
         def scale_weights():
-            scaled = keep.tile([P, O_TILES, SIDES, LANES, P], BF16)
-            for t in range(O_TILES):
-                for h in range(SIDES):
-                    nc.vector.tensor_tensor(
-                        out=scaled[:, t, h, :, :].rearrange("p l (k m) -> p l k m", m=FOLDED),
-                        in0=weight_sb[:, t, :].rearrange("p (k l h m) -> p h l k m", l=LANES, h=SIDES, m=FOLDED)[:, h],
-                        in1=scaler_wide[:, t, :, :].rearrange("p l (k m) -> p l k m", m=FOLDED),
-                        op=ALU.mult,
-                    )
+            scaled = keep.tile([P, SIDES, LANES, O_TILES, P], BF16)
+            weight_view = weight_sb[:].rearrange("p t (k l h m) -> p h l (t k) m", l=LANES, h=SIDES, m=FOLDED)
+            for h in range(SIDES):
+                nc.vector.tensor_tensor(
+                    out=scaled[:, h, :, :, :].rearrange("p l t (k m) -> p l (t k) m", m=FOLDED),
+                    in0=weight_view[:, h],
+                    in1=scaler_wide[:].rearrange("p l t (k m) -> p l (t k) m", m=FOLDED),
+                    op=ALU.mult,
+                )
             for t in range(O_TILES):
                 for h in range(SIDES):
                     for l in range(LANES):
-                        nc.tensor.transpose(flipped[:, t, h * LANES + l, :], scaled[:, t, h, l, :], identity[:])
+                        nc.tensor.transpose(flipped[:, t, h * LANES + l, :], scaled[:, h, l, t, :], identity[:])
 
         def group_weights():
             nc.scalar.copy(out=w_grouped[:], in_=flipped[:].rearrange("p t j o -> p t o j"))
@@ -339,12 +338,12 @@ def tile_kanv2d_s_kernel(tc, x, spline_weight, spline_scaler, out):
                     stop=True,
                 )
 
-        def leave(c, row, rows):
+        def leave(c, row, rows, copy=nc.scalar.copy):
             n, first = c // CHUNKS_PER_IMAGE, c % CHUNKS_PER_IMAGE * CHUNK_ROWS + row
             pixels = slice(first * PADDED, (first + rows) * PADDED)
             result = results.tile([P, O_TILES * N], F32, name="result")
             width = O_TILES * rows * PADDED
-            nc.scalar.copy(out=result[:, :width], in_=acc[c, row])
+            copy(out=result[:, :width], in_=acc[c, row])
             nc.sync.dma_start(
                 out=out[n, :, :, :].rearrange("(t o) y z -> o t (y z)", o=P)[:, :, pixels],
                 in_=result[:, :width].rearrange("o (t w) -> o t w", t=O_TILES),
@@ -392,10 +391,10 @@ def tile_kanv2d_s_kernel(tc, x, spline_weight, spline_scaler, out):
                 group_weights()
             if r + 3 in chunks:
                 far[r + 3] = far_distance(nc, work, x_view(r + 3, 1), shift)
-            if r + 1 in chunks and r + 1 not in masked:
-                sides[r + 1] = both_sides(nc, work, x_view(r + 1, 1), reach)
-            if r - STORE_LAG in chunks:
-                leave(r - STORE_LAG, 0, CHUNK_ROWS)
+            if r + 0 in chunks and r + 0 not in masked:
+                sides[r + 0] = both_sides(nc, work, x_view(r + 0, 1), reach)
+            for c in STORES.get(r, ()):
+                leave(c, 0, CHUNK_ROWS)
             folded[r] = folded_tile(r)
             if r == 0:
                 columns_a, columns_b = folded[0][:, : cut * LANES], folded[0][:, cut * LANES :]
@@ -436,7 +435,7 @@ def tile_kanv2d_s_kernel(tc, x, spline_weight, spline_scaler, out):
         for row in (0, half):
             quantise(last, row, half)
             multiply(last, row, half)
-        for c in range(last - STORE_LAG + 1, last):
+        for c in STORES.get(8, ()):
             leave(c, 0, CHUNK_ROWS)
-        for row in (0, half):
-            leave(last, row, half)
+        leave(last, 0, half, nc.vector.tensor_copy)
+        leave(last, half, half)

@@ -29,7 +29,7 @@ WIDTH = CHUNK_ROWS * SIDE * LANES
 O_TILES = COUT // P
 LOADS = ((0, 0, 2), (0, 2, 2), (1, 0, 4))
 MASK_GROUPS = ((0, 1), (2, 3), (4,))
-WARM_PASSES, WARM_COLUMNS = 4, 256
+WARM_PASSES, WARM_COLUMNS = 6, 256
 STORES = {4: (0,), 5: (1, 2), 6: (3,), 7: (4, 5), 8: (6,)}
 INV_SPACING = 2.5
 OUTER_ROOT = math.sqrt(1.0 / 6.0)
@@ -202,16 +202,23 @@ def tile_kanv2d_s_kernel(tc, x, spline_weight, spline_scaler, out):
         basis = keep.tile([P, BATCH, PADDED, PADDED, SIDES, LANES], BF16, align_bytes=64)
         pad_line = keep.tile([P, SIDES], F32)
         pad_basis = keep.tile([P, 1, 1, SIDES, LANES], BF16)
-        nc.vector.tensor_scalar(
-            out=pad_line[:], in0=reach[:], scalar1=11.0 / 24.0, scalar2=-5.0 / 24.0, op0=ALU.mult, op1=ALU.add
-        )
+        for h, sign in enumerate((1.0, -1.0)):
+            nc.vector.tensor_scalar(
+                out=pad_line[:, h : h + 1],
+                in0=pair_index[:],
+                scalar1=sign * 11.0 / 24.0,
+                scalar2=-sign * (FOLDED - 1) / 2.0 * 11.0 / 24.0 - 5.0 / 24.0,
+                op0=ALU.mult,
+                op1=ALU.add,
+            )
         nc.vector.tensor_scalar_max(
             out=pad_basis[:].rearrange("p r c h l -> p (r c h) l"),
             in0=pad_line[:].unsqueeze(2).to_broadcast([P, SIDES, LANES]),
             scalar1=0.0,
         )
         pad_word = pad_basis[:].rearrange("p r c h l -> p r c (h l)")
-        for n in range(BATCH):
+
+        def fill_ring(n):
             nc.vector.tensor_copy(
                 out=basis[:, n, 0 : PADDED : PADDED - 1, :, :, :].rearrange("p r c h l -> p r c (h l)"),
                 in_=pad_word.to_broadcast([P, 2, PADDED, PACK]),
@@ -365,19 +372,21 @@ def tile_kanv2d_s_kernel(tc, x, spline_weight, spline_scaler, out):
         xa, xb = x_view(0, 1)[:, :cut], x_view(0, 1)[:, cut:]
         far_a = far_distance(nc, work, xa, shift)
         far_b = far_distance(nc, work, xb, shift)
+        far[1] = far_distance(nc, work, x_view(1, 1), shift)
         dist_a = near_distance(nc, work, far_a)
         dist_b = near_distance(nc, work, far_b)
         outer_sq_a = outer_square(nc, work, dist_a)
         inner_sq_a = inner_square(nc, work, dist_a)
-        far[1] = far_distance(nc, work, x_view(1, 1), shift)
         outer_sq_b = outer_square(nc, work, dist_b)
         inner_sq_b = inner_square(nc, work, dist_b)
         dist[1] = near_distance(nc, work, far[1])
         far[2] = far_distance(nc, work, x_view(2, 1), shift)
+        fill_ring(0)
         make_upper(0)
+        fill_ring(1)
         widen_scaler()
-        scale_weights()
         make_lower(0)
+        scale_weights()
         make_upper(1)
         last = CHUNKS - 1
         for r in chunks:

@@ -93,6 +93,25 @@ def both_sides(nc, work, x_view, reach):
     return sides[:, :, :width]
 
 
+def upper_side(nc, work, x_view, reach):
+    width = x_view.shape[1] * x_view.shape[2]
+    sides = work.tile([P, SIDES, WIDTH], BF16, name="sides")
+    nc.scalar.activation(
+        out=sides[:, 1, :width].rearrange("p (w l) -> p w l", l=LANES),
+        in_=x_view,
+        func=ACT.Relu,
+        bias=reach[:, 1:2],
+        scale=INV_SPACING,
+    )
+    return sides[:, :, :width]
+
+
+def lower_side(nc, sides):
+    nc.vector.tensor_scalar(
+        out=sides[:, 0, :], in0=sides[:, 1, :], scalar1=0.0, scalar2=1.0, op0=ALU.is_le, op1=ALU.mult
+    )
+
+
 def upper_mask(nc, both, x_view, zero):
     nc.vector.tensor_scalar(
         out=both[:, 1, :].rearrange("p (w l) -> p w l", l=LANES),
@@ -400,8 +419,10 @@ def tile_kanv2d_s_kernel(tc, x, spline_weight, spline_scaler, out):
                 group_weights()
             if r + 3 in chunks:
                 far[r + 3] = far_distance(nc, work, x_view(r + 3, 1), shift)
-            if r + 0 in chunks and r + 0 not in masked:
-                sides[r + 0] = both_sides(nc, work, x_view(r + 0, 1), reach)
+            if r == last:
+                sides[r] = upper_side(nc, work, x_view(r, 1), reach)
+            elif r not in masked:
+                sides[r] = both_sides(nc, work, x_view(r, 1), reach)
             for c in STORES.get(r, ()):
                 leave(c, 0, CHUNK_ROWS)
             folded[r] = folded_tile(r)
@@ -439,6 +460,7 @@ def tile_kanv2d_s_kernel(tc, x, spline_weight, spline_scaler, out):
             if r > 1:
                 multiply(r - 1, 0, CHUNK_ROWS)
         clamp(nc, folded[last])
+        lower_side(nc, sides[last])
         unfold_rows(last, 0, half)
         unfold_rows(last, half, interior(last).shape[1])
         for row in (0, half):

@@ -30,7 +30,7 @@ O_TILES = COUT // P
 LOADS = ((0, 0, 2), (0, 2, 2), (1, 0, 4))
 MASK_GROUPS = ((0, 1), (2, 3), (4,))
 WARM_PASSES, WARM_COLUMNS = 6, 256
-STORES = {4: (0,), 5: (1, 2), 6: (3,), 7: (4, 5), 8: (6,)}
+STORES = {4: (0,), 5: (1,), 6: (2, 3), 7: (4, 5), 8: (6,)}
 INV_SPACING = 2.5
 OUTER_ROOT = math.sqrt(1.0 / 6.0)
 INNER_ROOT = math.sqrt(2.0 / 3.0)

import math

import concourse.mybir as mybir
from concourse.masks import make_identity

F32 = mybir.dt.float32
BF16 = mybir.dt.bfloat16
I32 = mybir.dt.int32
U32 = mybir.dt.uint32
U8 = mybir.dt.uint8
FP8X4 = mybir.dt.float8_e4m3fn_x4
ALU = mybir.AluOpType
ACT = mybir.ActivationFunctionType

P = 128
PACK = 4
BATCH, CIN, COUT, SIDE = 2, 64, 256, 30
BASES = 8
SIDES = 2
FOLDED = BASES // SIDES
LANES = PACK // SIDES
PAIRS = CIN // LANES
PADDED = SIDE + 2
CHUNK_ROWS = 8
N = CHUNK_ROWS * PADDED
CHUNKS_PER_IMAGE = PADDED // CHUNK_ROWS
CHUNKS = BATCH * CHUNKS_PER_IMAGE
WIDTH = CHUNK_ROWS * SIDE * LANES
O_TILES = COUT // P
LOADS = ((0, 0, 2), (0, 2, 2), (1, 0, 4))
MASK_GROUPS = ((0, 1), (2, 3), (4,))
WARM_PASSES, WARM_COLUMNS = 6, 256
STORES = {4: (0,), 5: (1,), 6: (2, 3), 7: (4, 5), 8: (6,)}
INV_SPACING = 2.5
OUTER_ROOT = math.sqrt(1.0 / 6.0)
INNER_ROOT = math.sqrt(2.0 / 3.0)

FLOPS = 2 * BATCH * PADDED * PADDED * CIN * BASES * COUT


def rows_of_x(n, chunk, chunks):
    first = chunk * CHUNK_ROWS
    return n, slice(max(1, first) - 1, min(PADDED - 1, first + chunks * CHUNK_ROWS) - 1)


def far_distance(nc, work, x_view, shift):
    width = x_view.shape[1] * x_view.shape[2]
    far = work.tile([P, WIDTH], F32, name="far")
    nc.scalar.activation(
        out=far[:, :width].rearrange("p (w l) -> p w l", l=LANES),
        in_=x_view,
        func=ACT.Abs,
        bias=shift,
        scale=INV_SPACING,
    )
    return far[:, :width]


def near_distance(nc, work, far):
    width = far.shape[1]
    dist = work.tile([P, WIDTH], F32, name="dist")
    nc.scalar.activation(out=dist[:, :width], in_=far, func=ACT.Abs, bias=-2.0, scale=1.0)
    return dist[:, :width]


def outer_square(nc, work, dist):
    width = dist.shape[1]
    outer_sq = work.tile([P, WIDTH], F32, name="outer_sq")
    nc.scalar.activation(
        out=outer_sq[:, :width], in_=dist, func=ACT.Square, bias=-2.0 * OUTER_ROOT, scale=OUTER_ROOT
    )
    return outer_sq[:, :width]


def inner_square(nc, work, dist):
    width = dist.shape[1]
    inner_sq = work.tile([P, WIDTH], F32, name="inner_sq")
    nc.scalar.activation(out=inner_sq[:, :width], in_=dist, func=ACT.Square, bias=-INNER_ROOT, scale=INNER_ROOT)
    return inner_sq[:, :width]


def both_sides(nc, work, x_view, reach):
    width = x_view.shape[1] * x_view.shape[2]
    sides = work.tile([P, SIDES, WIDTH], BF16, name="sides")
    for h, sign in enumerate((-1.0, 1.0)):
        nc.scalar.activation(
            out=sides[:, h, :width].rearrange("p (w l) -> p w l", l=LANES),
            in_=x_view,
            func=ACT.Relu,
            bias=reach[:, h : h + 1],
            scale=sign * INV_SPACING,
        )
    return sides[:, :, :width]


def upper_side(nc, work, x_view, reach):
    width = x_view.shape[1] * x_view.shape[2]
    sides = work.tile([P, SIDES, WIDTH], BF16, name="sides")
    nc.scalar.activation(
        out=sides[:, 1, :width].rearrange("p (w l) -> p w l", l=LANES),
        in_=x_view,
        func=ACT.Relu,
        bias=reach[:, 1:2],
        scale=INV_SPACING,
    )
    return sides[:, :, :width]


def lower_side(nc, sides):
    nc.vector.tensor_scalar(
        out=sides[:, 0, :], in0=sides[:, 1, :], scalar1=0.0, scalar2=1.0, op0=ALU.is_le, op1=ALU.mult
    )


def upper_mask(nc, both, x_view, zero):
    nc.vector.tensor_scalar(
        out=both[:, 1, :].rearrange("p (w l) -> p w l", l=LANES),
        in0=x_view,
        scalar1=zero,
        scalar2=1.0,
        op0=ALU.is_ge,
        op1=ALU.mult,
    )


def lower_mask(nc, both):
    nc.vector.tensor_scalar(
        out=both[:, 0, :], in0=both[:, 1, :], scalar1=-1.0, scalar2=1.0, op0=ALU.mult, op1=ALU.add
    )


def outer_product(nc, work, dist, outer_sq):
    width = dist.shape[1]
    outer_cube = work.tile([P, WIDTH], F32, name="outer_cube")
    nc.vector.scalar_tensor_tensor(
        out=outer_cube[:, :width], in0=dist, scalar=-2.0, in1=outer_sq, op0=ALU.add, op1=ALU.mult
    )
    return outer_cube[:, :width]


def inner_product(nc, work, dist, inner_sq):
    width = dist.shape[1]
    inner_cube = work.tile([P, WIDTH], F32, name="inner_cube")
    nc.vector.scalar_tensor_tensor(
        out=inner_cube[:, :width], in0=dist, scalar=-1.0, in1=inner_sq, op0=ALU.add, op1=ALU.mult
    )
    return inner_cube[:, :width]


def difference(nc, folded, outer_cube, inner_cube):
    nc.vector.scalar_tensor_tensor(
        out=folded, in0=inner_cube, scalar=0.0, in1=outer_cube, op0=ALU.min, op1=ALU.subtract
    )


def clamp(nc, folded):
    nc.vector.tensor_scalar_max(out=folded, in0=folded, scalar1=0.0)


def unfold(nc, folded, sides, out_view, op):
    rows, cols = out_view.shape[1], out_view.shape[2]
    nc.vector.tensor_tensor(
        out=out_view,
        in0=folded.rearrange("p (r c l) -> p r c l", r=rows, l=LANES)
        .unsqueeze(3)
        .to_broadcast([P, rows, cols, SIDES, LANES]),
        in1=sides.rearrange("p h (r c l) -> p r c h l", r=rows, l=LANES),
        op=op,
    )


def tile_kanv2d_s_kernel(tc, x, spline_weight, spline_scaler, out):
    nc = tc.nc
    with (
        tc.tile_pool(name="keep", bufs=1) as keep,
        tc.tile_pool(name="work", bufs=6) as work,
        tc.tile_pool(name="results", bufs=8) as results,
        tc.psum_pool(name="sums", bufs=8) as sums,
        tc.manual_schedule(),
    ):
        warm = keep.tile([P, 2], F32)
        nc.gpsimd.memset(warm[:, 0:1], 0.0)
        nc.scalar.activation(out=warm[:, 1:2], in_=warm[:, 0:1], func=ACT.Abs)
        partition_index = keep.tile([P, 1], I32)
        nc.gpsimd.iota(partition_index[:], pattern=[[0, 1]], base=0, channel_multiplier=1)

        weight_sb = keep.tile([P, O_TILES, CIN * BASES], BF16)
        scaler_sb = keep.tile([P, O_TILES, CIN], BF16)
        x_groups = []
        for g, load in enumerate(LOADS):
            n, x_rows = rows_of_x(*load)
            x_group = keep.tile([P, LANES, (x_rows.stop - x_rows.start) * SIDE], BF16, name="x%d" % g)
            x_groups.append((n, x_rows, x_group))
            for m in range(FOLDED):
                nc.sync.dma_start(
                    out=x_group[m:P:FOLDED, :, :],
                    in_=x[n, :, x_rows, :].rearrange("(k l) h w -> k l (h w)", l=LANES),
                )
            if g == 0:
                nc.sync.dma_start(out=scaler_sb[:], in_=spline_scaler.rearrange("(t p) i -> p t i", p=P))
                nc.sync.dma_start(
                    out=weight_sb[:], in_=spline_weight.rearrange("(t p) i g k l -> p t (i g k l)", p=P)
                )

        pair_index = keep.tile([P, 1], I32)
        nc.vector.tensor_single_scalar(out=pair_index[:], in_=partition_index[:], scalar=FOLDED - 1, op=ALU.bitwise_and)
        reach = keep.tile([P, SIDES], F32)
        for h, sign in enumerate((1.0, -1.0)):
            nc.vector.tensor_scalar(
                out=reach[:, h : h + 1],
                in0=pair_index[:],
                scalar1=sign,
                scalar2=-sign * (FOLDED - 1) / 2.0,
                op0=ALU.mult,
                op1=ALU.add,
            )
        shift = reach[:, 1:2]
        zero = keep.tile([P, 1], F32)
        nc.vector.tensor_scalar_mul(out=zero[:], in0=reach[:, 0:1], scalar1=1.0 / INV_SPACING)

        basis = keep.tile([P, BATCH, PADDED, PADDED, SIDES, LANES], BF16, align_bytes=64)
        pad_line = keep.tile([P, SIDES], F32)
        pad_basis = keep.tile([P, 1, 1, SIDES, LANES], BF16)
        for h, sign in enumerate((1.0, -1.0)):
            nc.vector.tensor_scalar(
                out=pad_line[:, h : h + 1],
                in0=pair_index[:],
                scalar1=sign * 11.0 / 24.0,
                scalar2=-sign * (FOLDED - 1) / 2.0 * 11.0 / 24.0 - 5.0 / 24.0,
                op0=ALU.mult,
                op1=ALU.add,
            )
        nc.vector.tensor_scalar_max(
            out=pad_basis[:].rearrange("p r c h l -> p (r c h) l"),
            in0=pad_line[:].unsqueeze(2).to_broadcast([P, SIDES, LANES]),
            scalar1=0.0,
        )
        pad_word = pad_basis[:].rearrange("p r c h l -> p r c (h l)")

        def fill_ring(n):
            nc.vector.tensor_copy(
                out=basis[:, n, 0 : PADDED : PADDED - 1, :, :, :].rearrange("p r c h l -> p r c (h l)"),
                in_=pad_word.to_broadcast([P, 2, PADDED, PACK]),
            )
            nc.vector.tensor_copy(
                out=basis[:, n, 1 : PADDED - 1, 0 : PADDED : PADDED - 1, :, :].rearrange("p r c h l -> p r c (h l)"),
                in_=pad_word.to_broadcast([P, PADDED - 2, 2, PACK]),
            )

        identity = keep.tile([P, P], BF16)
        make_identity(nc, identity[:])
        flipped = sums.tile([P, O_TILES, PACK, P], BF16, name="acc")
        scaler_wide = keep.tile([P, LANES, O_TILES, P], BF16)
        w_grouped = keep.tile([P, O_TILES, P, PACK], BF16, align_bytes=64)
        w_codes = keep.tile([P, COUT], U32, align_bytes=64)
        w_scales = keep.tile([P, COUT], U8, align_bytes=64)

        def widen_scaler():
            nc.gpsimd.tensor_scalar(
                out=scaler_wide[:].rearrange("p l t (k m) -> p l (t k) m", m=FOLDED),
                in0=scaler_sb[:]
                .rearrange("p t (k l) -> p l (t k)", l=LANES)
                .unsqueeze(3)
                .to_broadcast([P, LANES, O_TILES * PAIRS, FOLDED]),
                scalar1=1.0,
                scalar2=0.0,
                op0=ALU.mult,
                op1=ALU.add,
            )

        def scale_weights():
            scaled = keep.tile([P, SIDES, LANES, O_TILES, P], BF16)
            weight_view = weight_sb[:].rearrange("p t (k l h m) -> p h l (t k) m", l=LANES, h=SIDES, m=FOLDED)
            for h in range(SIDES):
                nc.vector.tensor_tensor(
                    out=scaled[:, h, :, :, :].rearrange("p l t (k m) -> p l (t k) m", m=FOLDED),
                    in0=weight_view[:, h],
                    in1=scaler_wide[:].rearrange("p l t (k m) -> p l (t k) m", m=FOLDED),
                    op=ALU.mult,
                )
            for t in range(O_TILES):
                for h in range(SIDES):
                    for l in range(LANES):
                        nc.tensor.transpose(flipped[:, t, h * LANES + l, :], scaled[:, h, l, t, :], identity[:])

        def group_weights():
            nc.scalar.copy(out=w_grouped[:], in_=flipped[:].rearrange("p t j o -> p t o j"))

        def quantise_weights():
            nc.vector.quantize_mx(
                out=w_codes[:].bitcast(FP8X4), scales=w_scales[:], in_=w_grouped[:].rearrange("p t o j -> p (t o j)")
            )

        b_codes = keep.tile([P, BATCH, PADDED * PADDED], U32, align_bytes=64)
        b_scales = keep.tile([P, BATCH, PADDED * PADDED], U8, align_bytes=64)
        chunks = range(CHUNKS)
        far, dist, outer_sq, inner_sq, outer_cube, inner_cube, folded, sides, acc = {}, {}, {}, {}, {}, {}, {}, {}, {}

        def x_view(c, count):
            n, wanted = rows_of_x(c // CHUNKS_PER_IMAGE, c % CHUNKS_PER_IMAGE, count)
            for image, x_rows, x_group in x_groups:
                if n == image and x_rows.start <= wanted.start < x_rows.stop:
                    columns = slice((wanted.start - x_rows.start) * SIDE, (wanted.stop - x_rows.start) * SIDE)
                    return x_group[:, :, columns].rearrange("p l w -> p w l")

        def columns_of(c):
            return x_view(c, 1).shape[1] * LANES

        def make_upper(g):
            group = MASK_GROUPS[g]
            upper_mask(nc, mask_tiles[g], x_view(group[0], len(group)), zero[:])

        def make_lower(g):
            lower_mask(nc, mask_tiles[g])

        def folded_tile(c):
            whole = work.tile([P, WIDTH], BF16, name="folded")
            return whole[:, : columns_of(c)]

        def interior(c):
            n, x_rows = rows_of_x(c // CHUNKS_PER_IMAGE, c % CHUNKS_PER_IMAGE, 1)
            return basis[:, n, x_rows.start + 1 : x_rows.stop + 1, 1 : 1 + SIDE, :, :]

        masked = [c for group in MASK_GROUPS for c in group]
        mask_tiles = []
        for group in MASK_GROUPS:
            both = keep.tile([P, SIDES, x_view(group[0], len(group)).shape[1] * LANES], BF16, name="masks%d" % group[0])
            mask_tiles.append(both)
            start = 0
            for c in group:
                sides[c] = both[:, :, start : start + columns_of(c)]
                start += columns_of(c)

        def unfold_rows(c, start, stop):
            columns = slice(start * SIDE * LANES, stop * SIDE * LANES)
            op = ALU.mult if c in masked else ALU.min
            unfold(nc, folded[c][:, columns], sides[c][:, :, columns], interior(c)[:, start:stop], op)

        def unfold_chunk(c):
            unfold_rows(c, 0, interior(c).shape[1])

        def quantise(c, row, rows):
            n, first = c // CHUNKS_PER_IMAGE, c % CHUNKS_PER_IMAGE * CHUNK_ROWS + row
            pixels = slice(first * PADDED, (first + rows) * PADDED)
            nc.vector.quantize_mx(
                out=b_codes[:, n, pixels].bitcast(FP8X4),
                scales=b_scales[:, n, pixels],
                in_=basis[:, n, first : first + rows, :, :, :].rearrange("p r c h l -> p (r c h l)"),
            )

        def multiply(c, row, rows):
            n, first = c // CHUNKS_PER_IMAGE, c % CHUNKS_PER_IMAGE * CHUNK_ROWS + row
            pixels = slice(first * PADDED, (first + rows) * PADDED)
            bank = sums.tile([P, O_TILES, N], F32, name="acc")
            acc[c, row] = bank[:].rearrange("p t w -> p (t w)")[:, : O_TILES * rows * PADDED]
            for t in range(O_TILES):
                nc.tensor.matmul_mx(
                    out=acc[c, row][:, t * rows * PADDED : (t + 1) * rows * PADDED],
                    lhsT=w_codes[:, t * P : (t + 1) * P].bitcast(FP8X4),
                    lhsT_scale=w_scales[:, t * P : (t + 1) * P],
                    rhs=b_codes[:, n, pixels].bitcast(FP8X4),
                    rhs_scale=b_scales[:, n, pixels],
                    start=True,
                    stop=True,
                )

        def leave(c, row, rows, copy=nc.scalar.copy):
            n, first = c // CHUNKS_PER_IMAGE, c % CHUNKS_PER_IMAGE * CHUNK_ROWS + row
            pixels = slice(first * PADDED, (first + rows) * PADDED)
            result = results.tile([P, O_TILES * N], F32, name="result")
            width = O_TILES * rows * PADDED
            copy(out=result[:, :width], in_=acc[c, row])
            nc.sync.dma_start(
                out=out[n, :, :, :].rearrange("(t o) y z -> o t (y z)", o=P)[:, :, pixels],
                in_=result[:, :width].rearrange("o (t w) -> o t w", t=O_TILES),
            )

        def keep_warm(values):
            idle_bank = sums.tile([P, O_TILES * N], F32, name="acc")
            for k in range(WARM_PASSES):
                nc.tensor.matmul(
                    out=idle_bank[:, :WARM_COLUMNS],
                    lhsT=identity[:],
                    rhs=values[:, :WARM_COLUMNS],
                    start=True,
                    stop=True,
                )

        half = CHUNK_ROWS // 2
        cut = (half - 1) * SIDE
        xa, xb = x_view(0, 1)[:, :cut], x_view(0, 1)[:, cut:]
        far_a = far_distance(nc, work, xa, shift)
        far_b = far_distance(nc, work, xb, shift)
        far[1] = far_distance(nc, work, x_view(1, 1), shift)
        dist_a = near_distance(nc, work, far_a)
        dist_b = near_distance(nc, work, far_b)
        outer_sq_a = outer_square(nc, work, dist_a)
        inner_sq_a = inner_square(nc, work, dist_a)
        outer_sq_b = outer_square(nc, work, dist_b)
        inner_sq_b = inner_square(nc, work, dist_b)
        dist[1] = near_distance(nc, work, far[1])
        far[2] = far_distance(nc, work, x_view(2, 1), shift)
        fill_ring(0)
        make_upper(0)
        fill_ring(1)
        widen_scaler()
        make_lower(0)
        scale_weights()
        make_upper(1)
        last = CHUNKS - 1
        for r in chunks:
            if r + 1 in chunks:
                outer_sq[r + 1] = outer_square(nc, work, dist[r + 1])
            if r + 2 in chunks:
                dist[r + 2] = near_distance(nc, work, far[r + 2])
            if r + 1 in chunks:
                inner_sq[r + 1] = inner_square(nc, work, dist[r + 1])
            if r == 1:
                group_weights()
            if r + 3 in chunks:
                far[r + 3] = far_distance(nc, work, x_view(r + 3, 1), shift)
            if r == last:
                sides[r] = upper_side(nc, work, x_view(r, 1), reach)
            elif r not in masked:
                sides[r] = both_sides(nc, work, x_view(r, 1), reach)
            for c in STORES.get(r, ()):
                leave(c, 0, CHUNK_ROWS)
            folded[r] = folded_tile(r)
            if r == 0:
                columns_a, columns_b = folded[0][:, : cut * LANES], folded[0][:, cut * LANES :]
                outer_cube_a = outer_product(nc, work, dist_a, outer_sq_a)
                inner_cube_a = inner_product(nc, work, dist_a, inner_sq_a)
                outer_cube_b = outer_product(nc, work, dist_b, outer_sq_b)
                difference(nc, columns_a, outer_cube_a, inner_cube_a)
                inner_cube_b = inner_product(nc, work, dist_b, inner_sq_b)
                make_lower(1)
                difference(nc, columns_b, outer_cube_b, inner_cube_b)
                make_upper(2)
                clamp(nc, folded[0])
                continue
            outer_cube[r] = outer_product(nc, work, dist[r], outer_sq[r])
            if r > 1:
                clamp(nc, folded[r - 1])
            else:
                make_lower(2)
                unfold_chunk(0)
            if r == last:
                keep_warm(folded[r - 1])
            inner_cube[r] = inner_product(nc, work, dist[r], inner_sq[r])
            if r > 1:
                unfold_chunk(r - 1)
            else:
                quantise(0, 0, CHUNK_ROWS)
            difference(nc, folded[r], outer_cube[r], inner_cube[r])
            if r > 1:
                quantise(r - 1, 0, CHUNK_ROWS)
            if r == 2:
                quantise_weights()
                multiply(0, 0, CHUNK_ROWS)
            if r > 1:
                multiply(r - 1, 0, CHUNK_ROWS)
        clamp(nc, folded[last])
        lower_side(nc, sides[last])
        unfold_rows(last, 0, half)
        unfold_rows(last, half, interior(last).shape[1])
        for row in (0, half):
            quantise(last, row, half)
            multiply(last, row, half)
        for c in STORES.get(8, ()):
            leave(c, 0, CHUNK_ROWS)
        leave(last, 0, half, nc.vector.tensor_copy)
        leave(last, half, half)
